import numpy as np
import ml_dtypes


def mxq(x, axis, fmt="e4m3"):
    dtype, down = {"e4m3": (ml_dtypes.float8_e4m3fn, 7), "e5m2": (ml_dtypes.float8_e5m2, 14)}[fmt]
    v = np.moveaxis(np.asarray(x, np.float32).astype(ml_dtypes.bfloat16).astype(np.float64), axis, -1)
    blocks = v.reshape(v.shape[:-1] + (-1, 32))
    amax = np.abs(blocks).max(-1, keepdims=True)
    byte = np.maximum(np.where(amax > 0, np.frexp(amax)[1] - 1 + 127, 0) - down, 1)
    scale = np.exp2(byte - 127.0)
    codes = (blocks / scale).astype(np.float32).astype(dtype).astype(np.float64)
    return np.moveaxis((codes * scale).reshape(v.shape), -1, axis)


WIDE = False


def mx_kscale(k):
    if not WIDE:
        return np.ones(k)
    levels = np.array([18, -18])
    if k % 512:
        return np.exp2(np.random.permutation(np.resize(levels, k // 32))).repeat(32)
    a = np.empty((k // 512, 16))
    for p in range(k // 512):
        a[p, :8] = np.random.permutation(np.resize(levels, 8))
        for g in range(8):
            far = levels[np.abs(levels - a[p, g]) >= 10]
            a[p, g + 8] = far[np.random.randint(len(far))]
    return np.exp2(a.ravel()).repeat(32)


BF16 = ml_dtypes.bfloat16


def bf(x):
    return np.asarray(x, np.float32).astype(BF16)


def f64(x):
    return np.asarray(x).astype(np.float64)


B, S, NS, DS, H = 8, 128, 2, 512, 1024
D = NS * DS
HALF = D // 2
T = B * S
EPS = 1e-6
ROPE_BASE = 10000.0


def sigmoid(v):
    return 1.0 / (1.0 + np.exp(-v))


def rope_cos_sin():
    inv_freq = 1.0 / ROPE_BASE ** (np.arange(0, D, 2) / D)
    freqs = np.arange(S)[:, None] * inv_freq[None, :]
    emb = np.concatenate([freqs, freqs], axis=-1)
    return np.cos(emb), np.sin(emb)


def rope(h):
    cos, sin = rope_cos_sin()
    rot = np.concatenate([-h[..., HALF:], h[..., :HALF]], axis=-1)
    return h * cos[None] + rot * sin[None]


def rope_back(dr):
    cos, sin = rope_cos_sin()
    rot = np.concatenate([dr[..., HALF:], -dr[..., :HALF]], axis=-1)
    return dr * cos[None] + rot * sin[None]


def forward_values(x, norm_w, Wg, Wu):
    xf = f64(x)
    rstd = 1.0 / np.sqrt(np.mean(xf * xf, axis=-1) + EPS)
    r = rope(xf * rstd[..., None] * f64(norm_w))
    rc = r.reshape(T, NS, DS).transpose(1, 0, 2)
    zg = (rc @ f64(Wg)).transpose(1, 0, 2).reshape(B, S, NS, H)
    zu = (rc @ f64(Wu)).transpose(1, 0, 2).reshape(B, S, NS, H)
    return zg, zu, rstd


def setup_inputs():
    s = mx_kscale(T).reshape(B, S)
    u = mx_kscale(H)
    x0 = bf(np.random.standard_normal((B, S, D)))
    norm_w = bf(1.0 + 0.1 * np.random.standard_normal(D))
    Wg0 = bf(np.random.standard_normal((NS, DS, H)) / np.sqrt(DS))
    Wu0 = bf(np.random.standard_normal((NS, DS, H)) / np.sqrt(DS))
    zg, zu, rstd = forward_values(x0, norm_w, Wg0, Wu0)
    g = bf(np.random.standard_normal((B, S, NS, H)) * np.exp2(np.random.randint(-6, 1, (B, S, 1, 1))) / s[:, :, None, None] * u)
    return {"x": bf(f64(x0) * s[:, :, None]),
            "norm_w": norm_w,
            "Wg": bf(f64(Wg0) / u),
            "Wu": bf(f64(Wu0) / u),
            "zg": np.asarray(zg, np.float32),
            "zu": np.asarray(zu, np.float32),
            "rstd": np.asarray(rstd, np.float32),
            "grad_out": g}


def reference(x, norm_w, Wg, Wu, zg, zu, rstd, grad_out):
    g = f64(grad_out)
    zgf = f64(zg)
    sg = sigmoid(zgf)
    dg = g * f64(zu) * (sg * (1.0 + zgf * (1.0 - sg)))
    du = g * (zgf * sg)
    dg = dg.reshape(T, NS, H).transpose(1, 0, 2)
    du = du.reshape(T, NS, H).transpose(1, 0, 2)
    dz = np.concatenate([dg, du], axis=2)
    W = np.concatenate([f64(Wg), f64(Wu)], axis=2)
    dr = mxq(dz, 2, "e5m2") @ mxq(W, 2, "e4m3").transpose(0, 2, 1)
    dh = rope_back(dr.transpose(1, 0, 2).reshape(B, S, D))
    rs = f64(rstd)[:, :, None]
    xhat = f64(x) * rs
    dn = dh * f64(norm_w)
    dx = rs * (dn - xhat * np.mean(dn * xhat, axis=-1, keepdims=True))
    rc = rope(xhat * f64(norm_w)).reshape(T, NS, DS).transpose(1, 0, 2)
    dWg = mxq(rc, 1, "e4m3").transpose(0, 2, 1) @ mxq(dg, 1, "e5m2")
    return dx, dWg

@@ -1,0 +1,402 @@
+import math
+from contextlib import ExitStack
+
+import concourse.mybir as mybir
+from concourse.masks import make_identity
+
+B, S, NS, DS, H = 8, 128, 2, 512, 1024
+D = NS * DS
+T = B * S
+FLOPS = 2 * NS * T * DS * 2 * H + 2 * NS * T * DS * H
+
+F32 = mybir.dt.float32
+BF16 = mybir.dt.bfloat16
+I32 = mybir.dt.int32
+U32 = mybir.dt.uint32
+U8 = mybir.dt.uint8
+E4 = mybir.dt.float8_e4m3fn_x4
+E5 = mybir.dt.float8_e5m2_x4
+ALU = mybir.AluOpType
+ACT = mybir.ActivationFunctionType
+
+P = 128
+PACK = 4
+KP = P * PACK
+NBLK = DS // P
+STEPS = 16
+
+
+def tile_mopn_layer_pa_v_kernel(tc, x, norm_w, Wg, Wu, zg, zu, rstd, grad_out, out_0, out_1):
+    nc = tc.nc
+    by_token = "b s n h -> (b s) (n h)"
+    tokens = "(g p j) w -> g p j w"
+    zg_v = zg.rearrange(by_token).rearrange(tokens, p=P, j=PACK)
+    zu_v = zu.rearrange(by_token).rearrange(tokens, p=P, j=PACK)
+    go_v = grad_out.rearrange(by_token).rearrange(tokens, p=P, j=PACK)
+    x_v = x.rearrange("b s d -> (b s) d").rearrange(tokens, p=P, j=PACK)
+    o0_v = out_0.rearrange("b s d -> (b s) d").rearrange(tokens, p=P, j=PACK)
+    weights = (Wg, Wu)
+
+    with ExitStack() as ctx:
+        keep = ctx.enter_context(tc.tile_pool(name="keep", bufs=1))
+        flow = ctx.enter_context(tc.tile_pool(name="flow", bufs=2))
+        psum = ctx.enter_context(tc.psum_pool(name="psum", bufs=8))
+        ctx.enter_context(tc.manual_schedule())
+
+        def bank():
+            return psum.tile([P, KP], F32, name="bank", tag="bank")
+
+        def work():
+            return flow.tile([P, 2, KP], F32, name="work", tag="work", bufs=9)
+
+        def grouped():
+            return flow.tile([P, KP * PACK], BF16, name="grouped", tag="grouped", bufs=6, align_bytes=64)
+
+        def quantize(src, fmt, tag, bufs):
+            codes = flow.tile([P, KP], U32, name=tag, tag=tag, bufs=bufs, align_bytes=64)
+            scales = flow.tile([P, KP], U8, name=tag + "_s", tag=tag + "_s", bufs=bufs, align_bytes=64)
+            nc.vector.quantize_mx(out=codes[:].bitcast(fmt), scales=scales[:], in_=src[:])
+            return codes, scales
+
+        ident = keep.tile([P, P], F32, name="ident")
+        rs = keep.tile([P, 2, PACK], F32, name="rs")
+        rs_sq = keep.tile([P, 2, PACK], F32, name="rs_sq")
+        tables = keep.tile([P, NBLK, 5, P], F32, name="tables")
+        sums = keep.tile([P, 2 * PACK, 8], F32, name="sums")
+        xs, zgs, zus, gos, ths, sil, dgs, dus = {}, {}, {}, {}, {}, {}, {}, {}
+        dzT, tok, raw_w, w_grp, w_q, dz_q, tok_q = {}, {}, {}, {}, {}, {}, {}
+        xhat, x_banks, r_prod, r_banks, r_grp, r_q = {}, {}, {}, {}, {}, {}
+        dr_banks, turned, dn_banks, res, dz_banks = {}, {}, {}, {}, {}
+
+        def place(i):
+            c, jp = divmod(i, 2)
+            return c // 4, slice(c % 4 * KP, (c % 4 + 1) * KP), slice(2 * jp, 2 * jp + 2)
+
+        def load_zg(i):
+            g, cols, js = place(i)
+            zgs[i] = flow.tile([P, 2, KP], F32, name="zg", tag="zg", bufs=3)
+            nc.sync.dma_start(out=zgs[i][:], in_=zg_v[g, :, js, cols])
+
+        def load_rest(i):
+            g, cols, js = place(i)
+            gos[i] = flow.tile([P, 2, KP], BF16, name="go", tag="go", bufs=3)
+            nc.sync.dma_start(out=gos[i][:], in_=go_v[g, :, js, cols])
+            zus[i] = flow.tile([P, 2, KP], F32, name="zu", tag="zu", bufs=3)
+            nc.sync.dma_start(out=zus[i][:], in_=zu_v[g, :, js, cols])
+
+        def load_x(g):
+            xs[g] = keep.tile([P, PACK, D], BF16, name="x%d" % g)
+            nc.sync.dma_start(out=xs[g][:], in_=x_v[g])
+
+        def load_w(k):
+            n, which, h2 = k // 4, k % 2, k % 4 // 2
+            raw_w[k] = flow.tile([P, NBLK, KP], BF16, name="raw_w", tag="raw_w")
+            rows = weights[which][n].rearrange("(b p) h -> p b h", p=P)
+            nc.sync.dma_start(out=raw_w[k][:], in_=rows[:, :, h2 * KP : (h2 + 1) * KP])
+
+        def turn_words(src, rows):
+            dst = bank()
+            view = dst[:].rearrange("p (u r m) -> p u r m", u=2, r=2)
+            words = src[:].bitcast(F32)
+            for u in range(2):
+                for r in range(2):
+                    nc.tensor.transpose(view[:, u, r, :], words[:, rows + r, u : 2 * P : 2], ident[:])
+            return dst
+
+        def empty_words(dst, half, src):
+            out = dst[:].bitcast(F32).rearrange("p (h m u) -> p h m u", h=2, u=2)[:, half]
+            nc.scalar.copy(out=out, in_=src[:].rearrange("p (u m) -> p m u", u=2))
+
+        def activations(i):
+            ths[i], sil[i] = work(), work()
+            nc.scalar.activation(out=ths[i][:], in_=zgs[i][:], func=ACT.Tanh, scale=0.5)
+            nc.scalar.activation(out=sil[i][:], in_=zgs[i][:], func=ACT.Silu, scale=-1.0)
+
+        def gate(i):
+            c, jp = divmod(i, 2)
+            if jp == 0:
+                dgs[c] = flow.tile([P, PACK, KP], BF16, name="dg", tag="dg")
+            dus[i] = flow.tile([P, 2, KP], BF16, name="du", tag="du")
+            stt = nc.vector.scalar_tensor_tensor
+            stt(out=ths[i][:], in0=ths[i][:], scalar=1.0, in1=gos[i][:], op0=ALU.add, op1=ALU.mult)
+            stt(out=sil[i][:], in0=sil[i][:], scalar=1.0, in1=zus[i][:], op0=ALU.subtract, op1=ALU.mult)
+            stt(out=dus[i][:], in0=ths[i][:], scalar=0.5, in1=zgs[i][:], op0=ALU.mult, op1=ALU.mult)
+            stt(out=dgs[c][:, 2 * jp : 2 * jp + 2, :], in0=ths[i][:], scalar=-0.5, in1=sil[i][:], op0=ALU.mult, op1=ALU.mult)
+
+        def turn_dz(i):
+            c, jp = divmod(i, 2)
+            dz_banks[i] = (turn_words(dus[i], 0), turn_words(dgs[c], 2 * jp))
+
+        def empty_dz(i):
+            c, jp = divmod(i, 2)
+            if jp == 0:
+                dzT[c] = (grouped(), grouped())
+            empty_words(dzT[c][1], jp, dz_banks[i][0])
+            if jp == 1:
+                tok[c] = grouped()
+                nc.scalar.copy(
+                    out=tok[c][:].rearrange("p (c i j) -> p c j i", i=4, j=PACK),
+                    in_=dgs[c][:].rearrange("p j (c i) -> p c j i", i=4),
+                )
+            empty_words(dzT[c][0], jp, dz_banks[i][1])
+
+        def quantize_dz(c):
+            dz_q[c] = [quantize(dzT[c][which], E5, "dz_q", 6) for which in range(2)]
+
+        def quantize_tok(c):
+            tok_q[c] = quantize(tok[c], E5, "tok_q", 6)
+
+        def turn_w(k):
+            w_grp[k] = grouped()
+            for half in range(2):
+                empty_words(w_grp[k], half, turn_words(raw_w[k], 2 * half))
+
+        def quantize_w(k):
+            w_q[k] = quantize(w_grp[k], E4, "w_q", 8)
+
+        def rotate(out, src, b, slot):
+            shape = [P, 2, PACK, 4, 32]
+            nc.vector.tensor_tensor(
+                out=out.rearrange("p s (j a q) -> p s j a q", j=PACK, a=4),
+                in0=src[:].rearrange("p (s j a q) -> p s j a q", s=1, j=PACK, a=4).to_broadcast(shape),
+                in1=tables[:, b, slot : slot + 2, :].rearrange("p s (j a q) -> p s j a q", j=PACK, a=1).to_broadcast(shape),
+                op=ALU.mult,
+            )
+
+        def add_turned(dst, first, second):
+            nc.tensor.matmul(dst, lhsT=first, rhs=ident[:], start=True, stop=False, is_transpose=True)
+            nc.tensor.matmul(dst, lhsT=second, rhs=ident[:], start=False, stop=True, is_transpose=True)
+
+        def scale_x(u):
+            g, b = divmod(u, NBLK)
+            xhat[u] = work()
+            dst = xhat[u][:].rearrange("p s (a c) -> p (s a) c", c=2 * P).rearrange("p j (h c) -> p j h c", h=2)
+            src = xs[g][:].rearrange("p j (h b c) -> p j h b c", h=2, c=P)
+            for j in range(PACK):
+                nc.scalar.activation(out=dst[:, j], in_=src[:, j, :, b, :], func=ACT.Copy, scale=rs[:, g, j : j + 1])
+
+        def turn_x(u):
+            src = xhat[u][:].rearrange("p s (a c) -> p (s a) c", c=2 * P)
+            x_banks[u] = (bank(), bank())
+            for half in range(2):
+                for j in range(PACK):
+                    nc.tensor.transpose(x_banks[u][half][:, j * P : (j + 1) * P], src[:, j, half * P : (half + 1) * P], ident[:])
+
+        def rotate_x(u):
+            r_prod[u] = (work(), work())
+            rotate(r_prod[u][0][:], x_banks[u][0], u % NBLK, 3)
+            rotate(r_prod[u][1][:], x_banks[u][1], u % NBLK, 1)
+
+        def add_r(u):
+            r_banks[u] = (bank(), bank())
+            for half in range(2):
+                for j in range(PACK):
+                    cols = slice(j * P, (j + 1) * P)
+                    add_turned(r_banks[u][half][:, cols], r_prod[u][0][:, 1 - half, cols], r_prod[u][1][:, half, cols])
+
+        def empty_r(u):
+            g, b = divmod(u, NBLK)
+            if b == 0:
+                r_grp[g] = (grouped(), grouped())
+            for half in range(2):
+                nc.scalar.copy(
+                    out=r_grp[g][half][:, b * KP : (b + 1) * KP].rearrange("p (c j) -> p c j", j=PACK),
+                    in_=r_banks[u][half][:].rearrange("p (j c) -> p c j", j=PACK),
+                )
+
+        def quantize_r(g):
+            r_q[g] = [quantize(r_grp[g][half], E4, "r_q", 4) for half in range(2)]
+
+        def mx(acc, lhs, cols, rhs, start, stop):
+            nc.tensor.matmul_mx(
+                out=acc[:], lhsT=lhs[0][:, cols].bitcast(E4), lhsT_scale=lhs[1][:, cols],
+                rhs=rhs[0][:].bitcast(E5), rhs_scale=rhs[1][:], start=start, stop=stop,
+            )
+
+        def matmul_dr(g, n, b):
+            dr_banks[g, n, b] = bank()
+            for k in range(4):
+                mx(dr_banks[g, n, b], w_q[4 * n + k], slice(b * P, (b + 1) * P), dz_q[4 * g + 2 * n + k // 2][k % 2], k == 0, k == 3)
+
+        def rotate_dr(g, n, b):
+            if b == 0:
+                turned[g, n] = flow.tile([P, NBLK, 2, KP], F32, name="turned", tag="turned")
+            rotate(turned[g, n][:, b], dr_banks[g, n, b], b, 2 * n)
+
+        def add_dn(g, j):
+            dn_banks[g, j] = (bank(), bank())
+            cols = slice(j * P, (j + 1) * P)
+            for b in range(NBLK):
+                for half in range(2):
+                    add_turned(dn_banks[g, j][half][:, b * P : (b + 1) * P], turned[g, 0][:, b, half, cols], turned[g, 1][:, b, 1 - half, cols])
+
+        def row_sums(g, j):
+            res[g, j] = work()
+            for half in range(2):
+                nc.vector.scalar_tensor_tensor(
+                    out=res[g, j][:, half, :], in0=dn_banks[g, j][half][:], scalar=rs_sq[:, g, j : j + 1],
+                    in1=xs[g][:, j, half * DS : (half + 1) * DS], op0=ALU.mult, op1=ALU.mult,
+                    accum_out=sums[:, PACK * g + j, half : half + 1],
+                )
+
+        def join_sums(g, j):
+            row = sums[:, PACK * g + j, :]
+            nc.vector.tensor_scalar(out=row[:, 2:3], in0=row[:, 0:1], scalar1=row[:, 1:2], scalar2=None, op0=ALU.add)
+
+        def finish_row(g, j):
+            for half in range(2):
+                nc.vector.scalar_tensor_tensor(
+                    out=res[g, j][:, half, :], in0=xs[g][:, j, half * DS : (half + 1) * DS], scalar=sums[:, PACK * g + j, 2:3],
+                    in1=dn_banks[g, j][half][:], op0=ALU.mult, op1=ALU.add,
+                )
+
+        def store_row(g, j, pieces=1):
+            row = res[g, j][:].rearrange("p s c -> p (s c)")
+            for k in range(pieces):
+                cols = slice(k * D // pieces, (k + 1) * D // pieces)
+                nc.scalar.activation(out=row[:, cols], in_=row[:, cols], func=ACT.Copy, scale=rs[:, g, j : j + 1])
+                nc.sync.dma_start(out=o0_v[g, :, j, cols], in_=row[:, cols])
+
+        def weight_grad(c, pair):
+            n, h2 = divmod(c, 2)
+            stage = work()
+            for s in range(2):
+                b = 2 * pair + s
+                acc = bank()
+                for g in range(2):
+                    mx(acc, r_q[g][n], slice(b * P, (b + 1) * P), tok_q[4 * g + c], g == 0, g == 1)
+                nc.scalar.copy(out=stage[:, s, :], in_=acc[:])
+            rows = out_1[n].rearrange("(b p) h -> p b h", p=P)
+            nc.sync.dma_start(out=rows[:, 2 * pair : 2 * pair + 2, h2 * KP : (h2 + 1) * KP], in_=stage[:])
+
+        w_rows = keep.tile([P, P], BF16, name="w_rows")
+        small = work()
+        freq_row, w_rows32, pos = small[:, 0, 0:P], small[:, 0, P : 2 * P], small[:, 0, 2 * P : 3 * P]
+        w_col = keep.tile([P, 16], F32, name="w_col")
+        nc.vector.memset(w_rows[:], 0.0)
+        nc.vector.memset(freq_row, 1.0)
+        load_zg(0)
+        nc.sync.dma_start(out=w_rows[0:8, :], in_=norm_w.rearrange("(c p) -> c p", p=P))
+        load_rest(0)
+        nc.sync.dma_start(out=rs[:], in_=rstd.rearrange("b s -> (b s)").rearrange("(g p j) -> p g j", p=P, j=PACK))
+        load_zg(1)
+        load_x(0)
+        load_rest(1)
+        nc.scalar.activation(out=w_col[:, 8:9], in_=small[:, 0, 0:1], func=ACT.Silu)
+        nc.gpsimd.iota(pos, pattern=[[1, PACK], [PACK, 32]], base=0, channel_multiplier=0, allow_small_or_imprecise_dtypes=True)
+        make_identity(nc, ident[:])
+        step = math.log(10000.0) / DS
+        for k in range(7):
+            w = 2**k
+            nc.vector.tensor_scalar(out=freq_row[:, w : 2 * w], in0=freq_row[:, 0:w], scalar1=math.exp(-step * w), scalar2=None, op0=ALU.mult)
+        freq_bank, w_bank = bank(), bank()
+        nc.tensor.transpose(freq_bank[:, 0:P], freq_row, ident[:])
+        nc.vector.tensor_copy(out=w_col[:, 9:10], in_=freq_bank[:, 0:1])
+        activations(0)
+        trig = work()
+        turns, whole = trig[:, 0, :], trig[:, 1, :].bitcast(I32)
+        for b in range(NBLK):
+            nc.vector.tensor_scalar(
+                out=turns[:, b * P : (b + 1) * P], in0=pos, scalar1=w_col[:, 9:10],
+                scalar2=math.exp(-step * P * b) / (2 * math.pi), op0=ALU.mult, op1=ALU.mult,
+            )
+        nc.vector.tensor_copy(out=whole, in_=turns)
+        nc.vector.tensor_tensor(out=turns, in0=turns, in1=whole, op=ALU.subtract)
+        nc.vector.tensor_copy(out=w_rows32, in_=w_rows[:])
+        nc.tensor.transpose(w_bank[:, 0:P], w_rows32, ident[:])
+        sin, cos = small[:, 1, :], trig[:, 1, :]
+        nc.scalar.activation(out=cos, in_=turns, func=ACT.Abs)
+        nc.scalar.activation(out=sin, in_=turns, func=ACT.Sin, scale=2 * math.pi)
+        nc.scalar.activation(out=cos, in_=cos, func=ACT.Sin, scale=-2 * math.pi, bias=math.pi / 2)
+
+        def fill_tables():
+            nc.vector.tensor_copy(out=w_col[:, 0:8], in_=w_bank[:, 0:8])
+            nc.vector.scalar_tensor_tensor(out=rs_sq[:], in0=rs[:], scalar=-1.0 / D, in1=rs[:], op0=ALU.mult, op1=ALU.mult)
+            for slot, (wave, sign, half) in enumerate(((cos, 1.0, 0), (sin, -1.0, 1), (cos, 1.0, 1), (sin, 1.0, 0), (cos, 1.0, 0))):
+                gain = w_col[:, NBLK * half : NBLK * (half + 1)].rearrange("p (b a) -> p b a", a=1).to_broadcast([P, NBLK, P])
+                nc.vector.scalar_tensor_tensor(
+                    out=tables[:, :, slot, :], in0=wave.rearrange("p (b c) -> p b c", c=P), scalar=sign, in1=gain, op0=ALU.mult, op1=ALU.mult
+                )
+
+        r_at = {1: 0, 2: 1, 3: 2, 4: 3, 5: 4, 8: 5, 9: 6, 10: 7}
+        dr_at = {6: [(0, 0, 0), (0, 0, 1)], 7: [(0, 0, 2), (0, 0, 3)], 10: [(0, 1, 0), (0, 1, 1)], 11: [(0, 1, 2), (0, 1, 3)]}
+        rows_at = {12: [0], 13: [1], 14: [2], 15: [3]}
+        grad_at = {12: [(0, 0), (0, 1)], 13: [(1, 0)], 14: [(1, 1)], 15: [(2, 0), (2, 1)]}
+
+        for i in range(STEPS):
+            if i + 2 < STEPS:
+                load_zg(i + 2)
+                load_rest(i + 2)
+            if i < 8:
+                load_w(i)
+            if i == 2:
+                load_x(1)
+            if i + 1 < STEPS:
+                activations(i + 1)
+            if i - 1 in r_at:
+                empty_r(r_at[i - 1])
+            if i + 1 in r_at:
+                scale_x(r_at[i + 1])
+            if i in r_at:
+                turn_x(r_at[i])
+            for key in dr_at.get(i, []):
+                matmul_dr(*key)
+            for j in rows_at.get(i, []):
+                add_dn(0, j)
+            if 1 <= i <= 8:
+                turn_w(i - 1)
+            for key in grad_at.get(i, []):
+                weight_grad(*key)
+            for j in rows_at.get(i, []):
+                row_sums(0, j)
+            gate(i)
+            if i == 0:
+                fill_tables()
+            for j in rows_at.get(i, []):
+                join_sums(0, j)
+            if i >= 2 and i % 2 == 0:
+                quantize_dz(i // 2 - 1)
+                quantize_tok(i // 2 - 1)
+            if 1 <= i <= 8:
+                quantize_w(i - 1)
+            if i - 1 in r_at and r_at[i - 1] % NBLK == NBLK - 1:
+                quantize_r(r_at[i - 1] // NBLK)
+            if i == STEPS - 1:
+                for b in range(2):
+                    matmul_dr(1, 0, b)
+            turn_dz(i)
+            for j in rows_at.get(i, []):
+                finish_row(0, j)
+            if i in r_at:
+                rotate_x(r_at[i])
+                add_r(r_at[i])
+            for key in dr_at.get(i, []):
+                rotate_dr(*key)
+            empty_dz(i)
+            for j in rows_at.get(i, []):
+                store_row(0, j)
+
+        for b in range(2, NBLK):
+            matmul_dr(1, 0, b)
+        for b in range(NBLK - 1):
+            rotate_dr(1, 0, b)
+        quantize_dz(7)
+        rotate_dr(1, 0, NBLK - 1)
+        for b in range(NBLK):
+            matmul_dr(1, 1, b)
+        for b in range(NBLK):
+            rotate_dr(1, 1, b)
+        quantize_tok(7)
+        add_dn(1, 0)
+        add_dn(1, 1)
+        weight_grad(3, 0)
+        weight_grad(3, 1)
+        row_sums(1, 0)
+        for j in range(PACK):
+            if j + 1 < PACK:
+                row_sums(1, j + 1)
+            join_sums(1, j)
+            finish_row(1, j)
+            if j + 2 < PACK:
+                add_dn(1, j + 2)
+            store_row(1, j, 2 if j == PACK - 1 else 1)

@@ -50,7 +50,7 @@ def tile_mopn_layer_pa_v_kernel(tc, x, norm_w, Wg, Wu, zg, zu, rstd, grad_out, o
             return flow.tile([P, 2, KP], F32, name="work", tag="work", bufs=9)
 
         def grouped():
-            return flow.tile([P, KP * PACK], BF16, name="grouped", tag="grouped", bufs=6, align_bytes=64)
+            return flow.tile([P, KP * PACK], BF16, name="grouped", tag="grouped", bufs=7, align_bytes=64)
 
         def quantize(src, fmt, tag, bufs):
             codes = flow.tile([P, KP], U32, name=tag, tag=tag, bufs=bufs, align_bytes=64)
@@ -59,6 +59,8 @@ def tile_mopn_layer_pa_v_kernel(tc, x, norm_w, Wg, Wu, zg, zu, rstd, grad_out, o
             return codes, scales
 
         ident = keep.tile([P, P], F32, name="ident")
+        ident16 = keep.tile([P, P], BF16, name="ident16")
+        rs_half = keep.tile([P, 2, PACK], F32, name="rs_half")
         rs = keep.tile([P, 2, PACK], F32, name="rs")
         rs_sq = keep.tile([P, 2, PACK], F32, name="rs_sq")
         tables = keep.tile([P, NBLK, 5, P], F32, name="tables")
@@ -66,6 +68,7 @@ def tile_mopn_layer_pa_v_kernel(tc, x, norm_w, Wg, Wu, zg, zu, rstd, grad_out, o
         xs, zgs, zus, gos, ths, sil, dgs, dus = {}, {}, {}, {}, {}, {}, {}, {}
         dzT, tok, raw_w, w_grp, w_q, dz_q, tok_q = {}, {}, {}, {}, {}, {}, {}
         xhat, x_banks, r_prod, r_banks, r_grp, r_q = {}, {}, {}, {}, {}, {}
+        go_banks = {}
         dr_banks, turned, dn_banks, res, dz_banks = {}, {}, {}, {}, {}
 
         def place(i):
@@ -79,7 +82,7 @@ def tile_mopn_layer_pa_v_kernel(tc, x, norm_w, Wg, Wu, zg, zu, rstd, grad_out, o
 
         def load_rest(i):
             g, cols, js = place(i)
-            gos[i] = flow.tile([P, 2, KP], BF16, name="go", tag="go", bufs=3)
+            gos[i] = flow.tile([P, 2, KP], BF16, name="go", tag="go", bufs=2)
             nc.sync.dma_start(out=gos[i][:], in_=go_v[g, :, js, cols])
             zus[i] = flow.tile([P, 2, KP], F32, name="zu", tag="zu", bufs=3)
             nc.sync.dma_start(out=zus[i][:], in_=zu_v[g, :, js, cols])
@@ -109,39 +112,54 @@ def tile_mopn_layer_pa_v_kernel(tc, x, norm_w, Wg, Wu, zg, zu, rstd, grad_out, o
 
         def activations(i):
             ths[i], sil[i] = work(), work()
-            nc.scalar.activation(out=ths[i][:], in_=zgs[i][:], func=ACT.Tanh, scale=0.5)
+            nc.scalar.activation(out=ths[i][:], in_=zgs[i][:], func=ACT.Tanh, scale=-0.5)
             nc.scalar.activation(out=sil[i][:], in_=zgs[i][:], func=ACT.Silu, scale=-1.0)
 
-        def gate(i):
+        def move_go(i):
+            go_banks[i] = psum.tile([P, 2, KP], BF16, name="bank", tag="bank")
+            for r in range(2):
+                nc.tensor.matmul(go_banks[i][:, r, :], lhsT=ident16[:], rhs=gos[i][:, r, :], start=True, stop=True)
+
+        def gate_common(i):
+            src = go_banks[i] if i in go_banks else gos[i]
+            nc.vector.scalar_tensor_tensor(out=ths[i][:], in0=ths[i][:], scalar=1.0, in1=src[:], op0=ALU.subtract, op1=ALU.mult)
+
+        def gate_du(i):
+            dus[i] = flow.tile([P, 2, KP], BF16, name="du", tag="du")
+            nc.vector.scalar_tensor_tensor(out=dus[i][:], in0=ths[i][:], scalar=-1.0, in1=zgs[i][:], op0=ALU.mult, op1=ALU.mult)
+
+        def gate_slope(i):
+            nc.vector.scalar_tensor_tensor(out=sil[i][:], in0=sil[i][:], scalar=1.0, in1=zus[i][:], op0=ALU.subtract, op1=ALU.mult)
+
+        def gate_dg(i, engine):
             c, jp = divmod(i, 2)
             if jp == 0:
                 dgs[c] = flow.tile([P, PACK, KP], BF16, name="dg", tag="dg")
-            dus[i] = flow.tile([P, 2, KP], BF16, name="du", tag="du")
-            stt = nc.vector.scalar_tensor_tensor
-            stt(out=ths[i][:], in0=ths[i][:], scalar=1.0, in1=gos[i][:], op0=ALU.add, op1=ALU.mult)
-            stt(out=sil[i][:], in0=sil[i][:], scalar=1.0, in1=zus[i][:], op0=ALU.subtract, op1=ALU.mult)
-            stt(out=dus[i][:], in0=ths[i][:], scalar=0.5, in1=zgs[i][:], op0=ALU.mult, op1=ALU.mult)
-            stt(out=dgs[c][:, 2 * jp : 2 * jp + 2, :], in0=ths[i][:], scalar=-0.5, in1=sil[i][:], op0=ALU.mult, op1=ALU.mult)
+            engine.tensor_tensor(out=dgs[c][:, 2 * jp : 2 * jp + 2, :], in0=ths[i][:], in1=sil[i][:], op=ALU.mult)
 
-        def turn_dz(i):
-            c, jp = divmod(i, 2)
-            dz_banks[i] = (turn_words(dus[i], 0), turn_words(dgs[c], 2 * jp))
+        def turn_du(i):
+            dz_banks[i, 1] = turn_words(dus[i], 0)
 
-        def empty_dz(i):
+        def turn_dg(i):
+            dz_banks[i, 0] = turn_words(dgs[i // 2], 2 * (i % 2))
+
+        def empty_dz(i, which):
             c, jp = divmod(i, 2)
             if jp == 0:
-                dzT[c] = (grouped(), grouped())
-            empty_words(dzT[c][1], jp, dz_banks[i][0])
-            if jp == 1:
-                tok[c] = grouped()
-                nc.scalar.copy(
-                    out=tok[c][:].rearrange("p (c i j) -> p c j i", i=4, j=PACK),
-                    in_=dgs[c][:].rearrange("p j (c i) -> p c j i", i=4),
-                )
-            empty_words(dzT[c][0], jp, dz_banks[i][1])
+                dzT[c, which] = grouped()
+            empty_words(dzT[c, which], jp, dz_banks[i, which])
 
-        def quantize_dz(c):
-            dz_q[c] = [quantize(dzT[c][which], E5, "dz_q", 6) for which in range(2)]
+        def interleave(c, half):
+            if half == 0:
+                tok[c] = grouped()
+            cols = slice(half * 64, (half + 1) * 64)
+            nc.scalar.copy(
+                out=tok[c][:].rearrange("p (c i j) -> p c j i", i=4, j=PACK)[:, cols],
+                in_=dgs[c][:].rearrange("p j (c i) -> p c j i", i=4)[:, cols],
+            )
+
+        def quantize_dz(c, which):
+            dz_q[c, which] = quantize(dzT[c, which], E5, "dz_q", 6)
 
         def quantize_tok(c):
             tok_q[c] = quantize(tok[c], E5, "tok_q", 6)
@@ -195,17 +213,23 @@ def tile_mopn_layer_pa_v_kernel(tc, x, norm_w, Wg, Wu, zg, zu, rstd, grad_out, o
                     add_turned(r_banks[u][half][:, cols], r_prod[u][0][:, 1 - half, cols], r_prod[u][1][:, half, cols])
 
         def empty_r(u):
-            g, b = divmod(u, NBLK)
-            if b == 0:
-                r_grp[g] = (grouped(), grouped())
+            r_grp[u] = flow.tile([P, 2, KP], BF16, name="r_grp", tag="r_grp", align_bytes=64)
             for half in range(2):
                 nc.scalar.copy(
-                    out=r_grp[g][half][:, b * KP : (b + 1) * KP].rearrange("p (c j) -> p c j", j=PACK),
+                    out=r_grp[u][:, half, :].rearrange("p (c j) -> p c j", j=PACK),
                     in_=r_banks[u][half][:].rearrange("p (j c) -> p c j", j=PACK),
                 )
 
-        def quantize_r(g):
-            r_q[g] = [quantize(r_grp[g][half], E4, "r_q", 4) for half in range(2)]
+        def quantize_r(u):
+            g, b = divmod(u, NBLK)
+            if b == 0:
+                codes = keep.tile([P, D], U32, name="r_codes%d" % g, align_bytes=64)
+                scales = keep.tile([P, D], U8, name="r_scales%d" % g, align_bytes=64)
+                r_q[g] = (codes, scales)
+            cols = slice(2 * b * P, 2 * (b + 1) * P)
+            nc.vector.quantize_mx(
+                out=r_q[g][0][:, cols].bitcast(E4), scales=r_q[g][1][:, cols], in_=r_grp[u][:].rearrange("p s c -> p (s c)")
+            )
 
         def mx(acc, lhs, cols, rhs, start, stop):
             nc.tensor.matmul_mx(
@@ -213,10 +237,11 @@ def tile_mopn_layer_pa_v_kernel(tc, x, norm_w, Wg, Wu, zg, zu, rstd, grad_out, o
                 rhs=rhs[0][:].bitcast(E5), rhs_scale=rhs[1][:], start=start, stop=stop,
             )
 
-        def matmul_dr(g, n, b):
-            dr_banks[g, n, b] = bank()
-            for k in range(4):
-                mx(dr_banks[g, n, b], w_q[4 * n + k], slice(b * P, (b + 1) * P), dz_q[4 * g + 2 * n + k // 2][k % 2], k == 0, k == 3)
+        def matmul_dr(g, n, b, passes=range(4)):
+            if 0 in passes:
+                dr_banks[g, n, b] = bank()
+            for k in passes:
+                mx(dr_banks[g, n, b], w_q[4 * n + k], slice(b * P, (b + 1) * P), dz_q[4 * g + 2 * n + k // 2, k % 2], k == 0, k == 3)
 
         def rotate_dr(g, n, b):
             if b == 0:
@@ -254,7 +279,7 @@ def tile_mopn_layer_pa_v_kernel(tc, x, norm_w, Wg, Wu, zg, zu, rstd, grad_out, o
             row = res[g, j][:].rearrange("p s c -> p (s c)")
             for k in range(pieces):
                 cols = slice(k * D // pieces, (k + 1) * D // pieces)
-                nc.scalar.activation(out=row[:, cols], in_=row[:, cols], func=ACT.Copy, scale=rs[:, g, j : j + 1])
+                nc.scalar.activation(out=row[:, cols], in_=row[:, cols], func=ACT.Copy, scale=rs_half[:, g, j : j + 1])
                 nc.sync.dma_start(out=o0_v[g, :, j, cols], in_=row[:, cols])
 
         def weight_grad(c, pair):
@@ -264,8 +289,8 @@ def tile_mopn_layer_pa_v_kernel(tc, x, norm_w, Wg, Wu, zg, zu, rstd, grad_out, o
                 b = 2 * pair + s
                 acc = bank()
                 for g in range(2):
-                    mx(acc, r_q[g][n], slice(b * P, (b + 1) * P), tok_q[4 * g + c], g == 0, g == 1)
-                nc.scalar.copy(out=stage[:, s, :], in_=acc[:])
+                    mx(acc, r_q[g], slice((2 * b + n) * P, (2 * b + n + 1) * P), tok_q[4 * g + c], g == 0, g == 1)
+                nc.scalar.activation(out=stage[:, s, :], in_=acc[:], func=ACT.Copy, scale=0.5)
             rows = out_1[n].rearrange("(b p) h -> p b h", p=P)
             nc.sync.dma_start(out=rows[:, 2 * pair : 2 * pair + 2, h2 * KP : (h2 + 1) * KP], in_=stage[:])
 
@@ -285,6 +310,7 @@ def tile_mopn_layer_pa_v_kernel(tc, x, norm_w, Wg, Wu, zg, zu, rstd, grad_out, o
         nc.scalar.activation(out=w_col[:, 8:9], in_=small[:, 0, 0:1], func=ACT.Silu)
         nc.gpsimd.iota(pos, pattern=[[1, PACK], [PACK, 32]], base=0, channel_multiplier=0, allow_small_or_imprecise_dtypes=True)
         make_identity(nc, ident[:])
+        nc.gpsimd.tensor_copy(out=ident16[:], in_=ident[:])
         step = math.log(10000.0) / DS
         for k in range(7):
             w = 2**k
@@ -310,6 +336,7 @@ def tile_mopn_layer_pa_v_kernel(tc, x, norm_w, Wg, Wu, zg, zu, rstd, grad_out, o
         nc.scalar.activation(out=cos, in_=cos, func=ACT.Sin, scale=-2 * math.pi, bias=math.pi / 2)
 
         def fill_tables():
+            nc.vector.tensor_scalar(out=rs_half[:], in0=rs[:], scalar1=0.5, scalar2=None, op0=ALU.mult)
             nc.vector.tensor_copy(out=w_col[:, 0:8], in_=w_bank[:, 0:8])
             nc.vector.scalar_tensor_tensor(out=rs_sq[:], in0=rs[:], scalar=-1.0 / D, in1=rs[:], op0=ALU.mult, op1=ALU.mult)
             for slot, (wave, sign, half) in enumerate(((cos, 1.0, 0), (sin, -1.0, 1), (cos, 1.0, 1), (sin, 1.0, 0), (cos, 1.0, 0))):
@@ -319,78 +346,112 @@ def tile_mopn_layer_pa_v_kernel(tc, x, norm_w, Wg, Wu, zg, zu, rstd, grad_out, o
                 )
 
         r_at = {1: 0, 2: 1, 3: 2, 4: 3, 5: 4, 8: 5, 9: 6, 10: 7}
-        dr_at = {6: [(0, 0, 0), (0, 0, 1)], 7: [(0, 0, 2), (0, 0, 3)], 10: [(0, 1, 0), (0, 1, 1)], 11: [(0, 1, 2), (0, 1, 3)]}
+        dr_at = {6: [(0, 0, 0), (0, 0, 1)], 7: [(0, 0, 2), (0, 0, 3)], 10: [(0, 1, 0)], 11: [(0, 1, 1), (0, 1, 2), (0, 1, 3)], 16: [(1, 0, 0), (1, 0, 1)]}
         rows_at = {12: [0], 13: [1], 14: [2], 15: [3]}
-        grad_at = {12: [(0, 0), (0, 1)], 13: [(1, 0)], 14: [(1, 1)], 15: [(2, 0), (2, 1)]}
+        grad_at = {13: [(0, 0), (0, 1)], 14: [(1, 0)], 15: [(1, 1)]}
 
-        for i in range(STEPS):
-            if i + 2 < STEPS:
-                load_zg(i + 2)
-                load_rest(i + 2)
-            if i < 8:
-                load_w(i)
-            if i == 2:
-                load_x(1)
-            if i + 1 < STEPS:
-                activations(i + 1)
-            if i - 1 in r_at:
-                empty_r(r_at[i - 1])
-            if i + 1 in r_at:
-                scale_x(r_at[i + 1])
+        def feed(i):
             if i in r_at:
                 turn_x(r_at[i])
             for key in dr_at.get(i, []):
                 matmul_dr(*key)
             for j in rows_at.get(i, []):
                 add_dn(0, j)
+
+        scale_x(0)
+        gate_common(0)
+        for i in range(STEPS):
+            last = i == STEPS - 1
+            rows = rows_at.get(i, [])
+            if i + 2 < STEPS:
+                load_zg(i + 2)
+            if i < 8:
+                load_w(i)
+            if i == 2:
+                load_x(1)
+            if not last:
+                activations(i + 1)
+            if i - 1 in r_at:
+                add_r(r_at[i - 1])
+                empty_r(r_at[i - 1])
+            if i >= 1:
+                turn_dg(i - 1)
+                empty_dz(i - 1, 0)
+            if not last:
+                move_go(i + 1)
+            if i + 2 < STEPS:
+                load_rest(i + 2)
+            gate_du(i)
+            turn_du(i)
+            empty_dz(i, 1)
             if 1 <= i <= 8:
                 turn_w(i - 1)
-            for key in grad_at.get(i, []):
-                weight_grad(*key)
-            for j in rows_at.get(i, []):
-                row_sums(0, j)
-            gate(i)
+            if i >= 2:
+                interleave(i // 2 - 1, i % 2)
+            if i + 2 in r_at:
+                scale_x(r_at[i + 2])
+            if 2 <= i <= 9:
+                quantize_w(i - 2)
+            if i - 2 in r_at:
+                quantize_r(r_at[i - 2])
+            if i >= 2 and i % 2 == 0:
+                quantize_dz(i // 2 - 1, 1)
+            if i >= 4 and i % 2 == 0:
+                quantize_tok(i // 2 - 2)
+            if i >= 3 and i % 2 == 1:
+                quantize_dz(i // 2 - 1, 0)
+            gate_slope(i)
             if i == 0:
                 fill_tables()
-            for j in rows_at.get(i, []):
-                join_sums(0, j)
-            if i >= 2 and i % 2 == 0:
-                quantize_dz(i // 2 - 1)
-                quantize_tok(i // 2 - 1)
-            if 1 <= i <= 8:
-                quantize_w(i - 1)
-            if i - 1 in r_at and r_at[i - 1] % NBLK == NBLK - 1:
-                quantize_r(r_at[i - 1] // NBLK)
-            if i == STEPS - 1:
-                for b in range(2):
-                    matmul_dr(1, 0, b)
-            turn_dz(i)
-            for j in rows_at.get(i, []):
-                finish_row(0, j)
+            if last:
+                row_sums(0, PACK - 1)
+            gate_dg(i, nc.vector if i == 0 or last else nc.gpsimd)
+            units = [lambda key=key: rotate_dr(*key) for key in dr_at.get(i, [])]
             if i in r_at:
-                rotate_x(r_at[i])
-                add_r(r_at[i])
-            for key in dr_at.get(i, []):
-                rotate_dr(*key)
-            empty_dz(i)
-            for j in rows_at.get(i, []):
+                r_prod[r_at[i]] = (work(), work())
+                units = [lambda h=h: rotate(r_prod[r_at[i]][h][:], x_banks[r_at[i]][h], r_at[i] % NBLK, 3 - 2 * h) for h in range(2)] + units
+            if rows and not last:
+                row_sums(0, rows[0])
+                gate_common(i + 1)
+            elif not last:
+                for unit in units[:-1]:
+                    unit()
+                gate_common(i + 1)
+                for unit in units[-1:]:
+                    unit()
+            for j in rows:
+                join_sums(0, j)
+                finish_row(0, j)
+            feed(i + 1)
+            for key in grad_at.get(i, []):
+                weight_grad(*key)
+            for j in rows:
                 store_row(0, j)
 
+        turn_dg(STEPS - 1)
+        empty_dz(STEPS - 1, 0)
         for b in range(2, NBLK):
             matmul_dr(1, 0, b)
-        for b in range(NBLK - 1):
-            rotate_dr(1, 0, b)
-        quantize_dz(7)
-        rotate_dr(1, 0, NBLK - 1)
+        for half in range(2):
+            interleave(7, half)
+        quantize_tok(6)
         for b in range(NBLK):
+            if b == 2:
+                quantize_dz(7, 1)
+                quantize_dz(7, 0)
+            rotate_dr(1, 0, b)
+            if b < 2:
+                matmul_dr(1, 1, b, range(2))
+        for b in range(2):
+            matmul_dr(1, 1, b, range(2, 4))
+        for b in range(2, NBLK):
             matmul_dr(1, 1, b)
+        weight_grad(2, 0)
         for b in range(NBLK):
             rotate_dr(1, 1, b)
         quantize_tok(7)
         add_dn(1, 0)
         add_dn(1, 1)
-        weight_grad(3, 0)
-        weight_grad(3, 1)
         row_sums(1, 0)
         for j in range(PACK):
             if j + 1 < PACK:
@@ -399,4 +460,9 @@ def tile_mopn_layer_pa_v_kernel(tc, x, norm_w, Wg, Wu, zg, zu, rstd, grad_out, o
             finish_row(1, j)
             if j + 2 < PACK:
                 add_dn(1, j + 2)
+            if j == 0:
+                weight_grad(2, 1)
+            if j == 1:
+                weight_grad(3, 0)
+                weight_grad(3, 1)
             store_row(1, j, 2 if j == PACK - 1 else 1)

@@ -80,10 +80,13 @@ def tile_mopn_layer_pa_v_kernel(tc, x, norm_w, Wg, Wu, zg, zu, rstd, grad_out, o
             zgs[i] = flow.tile([P, 2, KP], F32, name="zg", tag="zg", bufs=3)
             nc.sync.dma_start(out=zgs[i][:], in_=zg_v[g, :, js, cols])
 
-        def load_rest(i):
+        def load_go(i):
             g, cols, js = place(i)
             gos[i] = flow.tile([P, 2, KP], BF16, name="go", tag="go", bufs=2)
             nc.sync.dma_start(out=gos[i][:], in_=go_v[g, :, js, cols])
+
+        def load_zu(i):
+            g, cols, js = place(i)
             zus[i] = flow.tile([P, 2, KP], F32, name="zu", tag="zu", bufs=3)
             nc.sync.dma_start(out=zus[i][:], in_=zu_v[g, :, js, cols])
 
@@ -120,9 +123,9 @@ def tile_mopn_layer_pa_v_kernel(tc, x, norm_w, Wg, Wu, zg, zu, rstd, grad_out, o
             for r in range(2):
                 nc.tensor.matmul(go_banks[i][:, r, :], lhsT=ident16[:], rhs=gos[i][:, r, :], start=True, stop=True)
 
-        def gate_common(i):
+        def gate_common(i, js=slice(0, 2)):
             src = go_banks[i] if i in go_banks else gos[i]
-            nc.vector.scalar_tensor_tensor(out=ths[i][:], in0=ths[i][:], scalar=1.0, in1=src[:], op0=ALU.subtract, op1=ALU.mult)
+            nc.vector.scalar_tensor_tensor(out=ths[i][:, js], in0=ths[i][:, js], scalar=1.0, in1=src[:, js], op0=ALU.subtract, op1=ALU.mult)
 
         def gate_du(i):
             dus[i] = flow.tile([P, 2, KP], BF16, name="du", tag="du")
@@ -248,12 +251,15 @@ def tile_mopn_layer_pa_v_kernel(tc, x, norm_w, Wg, Wu, zg, zu, rstd, grad_out, o
                 turned[g, n] = flow.tile([P, NBLK, 2, KP], F32, name="turned", tag="turned")
             rotate(turned[g, n][:, b], dr_banks[g, n, b], b, 2 * n)
 
+        def add_dn_block(g, j, b):
+            cols = slice(j * P, (j + 1) * P)
+            for half in range(2):
+                add_turned(dn_banks[g, j][half][:, b * P : (b + 1) * P], turned[g, 0][:, b, half, cols], turned[g, 1][:, b, 1 - half, cols])
+
         def add_dn(g, j):
             dn_banks[g, j] = (bank(), bank())
-            cols = slice(j * P, (j + 1) * P)
             for b in range(NBLK):
-                for half in range(2):
-                    add_turned(dn_banks[g, j][half][:, b * P : (b + 1) * P], turned[g, 0][:, b, half, cols], turned[g, 1][:, b, 1 - half, cols])
+                add_dn_block(g, j, b)
 
         def row_sums(g, j):
             res[g, j] = work()
@@ -297,17 +303,20 @@ def tile_mopn_layer_pa_v_kernel(tc, x, norm_w, Wg, Wu, zg, zu, rstd, grad_out, o
         w_rows = keep.tile([P, P], BF16, name="w_rows")
         small = work()
         freq_row, w_rows32, pos = small[:, 0, 0:P], small[:, 0, P : 2 * P], small[:, 0, 2 * P : 3 * P]
-        w_col = keep.tile([P, 16], F32, name="w_col")
+        freq_col = keep.tile([P, 1], F32, name="freq_col")
         nc.vector.memset(w_rows[:], 0.0)
         nc.vector.memset(freq_row, 1.0)
-        load_zg(0)
+        zgs[0] = flow.tile([P, 2, KP], F32, name="zg", tag="zg", bufs=3)
+        nc.sync.dma_start(out=zgs[0][:, 0, :], in_=zg_v[0, :, 0, 0:KP])
+        load_go(0)
+        nc.sync.dma_start(out=zgs[0][:, 1, :], in_=zg_v[0, :, 1, 0:KP])
         nc.sync.dma_start(out=w_rows[0:8, :], in_=norm_w.rearrange("(c p) -> c p", p=P))
-        load_rest(0)
+        load_zu(0)
         nc.sync.dma_start(out=rs[:], in_=rstd.rearrange("b s -> (b s)").rearrange("(g p j) -> p g j", p=P, j=PACK))
         load_zg(1)
+        load_go(1)
         load_x(0)
-        load_rest(1)
-        nc.scalar.activation(out=w_col[:, 8:9], in_=small[:, 0, 0:1], func=ACT.Silu)
+        load_zu(1)
         nc.gpsimd.iota(pos, pattern=[[1, PACK], [PACK, 32]], base=0, channel_multiplier=0, allow_small_or_imprecise_dtypes=True)
         make_identity(nc, ident[:])
         nc.gpsimd.tensor_copy(out=ident16[:], in_=ident[:])
@@ -317,17 +326,21 @@ def tile_mopn_layer_pa_v_kernel(tc, x, norm_w, Wg, Wu, zg, zu, rstd, grad_out, o
             nc.vector.tensor_scalar(out=freq_row[:, w : 2 * w], in0=freq_row[:, 0:w], scalar1=math.exp(-step * w), scalar2=None, op0=ALU.mult)
         freq_bank, w_bank = bank(), bank()
         nc.tensor.transpose(freq_bank[:, 0:P], freq_row, ident[:])
-        nc.vector.tensor_copy(out=w_col[:, 9:10], in_=freq_bank[:, 0:1])
-        activations(0)
+        nc.vector.tensor_copy(out=freq_col[:], in_=freq_bank[:, 0:1])
+        ths[0], sil[0] = work(), work()
+        for func, scale, dst, r in ((ACT.Silu, -1.0, sil, 0), (ACT.Tanh, -0.5, ths, 0), (ACT.Tanh, -0.5, ths, 1), (ACT.Silu, -1.0, sil, 1)):
+            nc.scalar.activation(out=dst[0][:, r, :], in_=zgs[0][:, r, :], func=func, scale=scale)
         trig = work()
         turns, whole = trig[:, 0, :], trig[:, 1, :].bitcast(I32)
         for b in range(NBLK):
             nc.vector.tensor_scalar(
-                out=turns[:, b * P : (b + 1) * P], in0=pos, scalar1=w_col[:, 9:10],
+                out=turns[:, b * P : (b + 1) * P], in0=pos, scalar1=freq_col[:],
                 scalar2=math.exp(-step * P * b) / (2 * math.pi), op0=ALU.mult, op1=ALU.mult,
             )
         nc.vector.tensor_copy(out=whole, in_=turns)
+        gate_common(0, slice(0, 1))
         nc.vector.tensor_tensor(out=turns, in0=turns, in1=whole, op=ALU.subtract)
+        gate_common(0, slice(1, 2))
         nc.vector.tensor_copy(out=w_rows32, in_=w_rows[:])
         nc.tensor.transpose(w_bank[:, 0:P], w_rows32, ident[:])
         sin, cos = small[:, 1, :], trig[:, 1, :]
@@ -336,19 +349,16 @@ def tile_mopn_layer_pa_v_kernel(tc, x, norm_w, Wg, Wu, zg, zu, rstd, grad_out, o
         nc.scalar.activation(out=cos, in_=cos, func=ACT.Sin, scale=-2 * math.pi, bias=math.pi / 2)
 
         def fill_tables():
-            nc.vector.tensor_scalar(out=rs_half[:], in0=rs[:], scalar1=0.5, scalar2=None, op0=ALU.mult)
-            nc.vector.tensor_copy(out=w_col[:, 0:8], in_=w_bank[:, 0:8])
-            nc.vector.scalar_tensor_tensor(out=rs_sq[:], in0=rs[:], scalar=-1.0 / D, in1=rs[:], op0=ALU.mult, op1=ALU.mult)
-            for slot, (wave, sign, half) in enumerate(((cos, 1.0, 0), (sin, -1.0, 1), (cos, 1.0, 1), (sin, 1.0, 0), (cos, 1.0, 0))):
-                gain = w_col[:, NBLK * half : NBLK * (half + 1)].rearrange("p (b a) -> p b a", a=1).to_broadcast([P, NBLK, P])
+            for slot, (wave, sign, half) in enumerate(((sin, -1.0, 1), (sin, 1.0, 0), (cos, 1.0, 0), (cos, 1.0, 1), (cos, 1.0, 0))):
+                gain = w_bank[:, NBLK * half : NBLK * (half + 1)].rearrange("p (b a) -> p b a", a=1).to_broadcast([P, NBLK, P])
                 nc.vector.scalar_tensor_tensor(
-                    out=tables[:, :, slot, :], in0=wave.rearrange("p (b c) -> p b c", c=P), scalar=sign, in1=gain, op0=ALU.mult, op1=ALU.mult
+                    out=tables[:, :, (1, 3, 0, 2, 4)[slot], :], in0=wave.rearrange("p (b c) -> p b c", c=P), scalar=sign, in1=gain, op0=ALU.mult, op1=ALU.mult
                 )
 
-        r_at = {1: 0, 2: 1, 3: 2, 4: 3, 5: 4, 8: 5, 9: 6, 10: 7}
-        dr_at = {6: [(0, 0, 0), (0, 0, 1)], 7: [(0, 0, 2), (0, 0, 3)], 10: [(0, 1, 0)], 11: [(0, 1, 1), (0, 1, 2), (0, 1, 3)], 16: [(1, 0, 0), (1, 0, 1)]}
-        rows_at = {12: [0], 13: [1], 14: [2], 15: [3]}
-        grad_at = {13: [(0, 0), (0, 1)], 14: [(1, 0)], 15: [(1, 1)]}
+        r_at = {1: 0, 2: 1, 3: 2, 4: 3, 5: 4, 8: 5, 9: 6, 11: 7}
+        dr_at = {6: [(0, 0, 0), (0, 0, 1)], 7: [(0, 0, 2), (0, 0, 3)], 10: [(0, 1, b) for b in range(NBLK)], 15: [(1, 0, 0), (1, 0, 1)]}
+        rows_at = {11: [0], 12: [1], 13: [2], 14: [3]}
+        grad_at = {13: [(0, 0), (0, 1)], 14: [(1, 0), (1, 1)], 15: [(2, 0), (2, 1)]}
 
         def feed(i):
             if i in r_at:
@@ -358,8 +368,6 @@ def tile_mopn_layer_pa_v_kernel(tc, x, norm_w, Wg, Wu, zg, zu, rstd, grad_out, o
             for j in rows_at.get(i, []):
                 add_dn(0, j)
 
-        scale_x(0)
-        gate_common(0)
         for i in range(STEPS):
             last = i == STEPS - 1
             rows = rows_at.get(i, [])
@@ -369,8 +377,14 @@ def tile_mopn_layer_pa_v_kernel(tc, x, norm_w, Wg, Wu, zg, zu, rstd, grad_out, o
                 load_w(i)
             if i == 2:
                 load_x(1)
-            if not last:
+            if last:
+                interleave(6, 1)
+            else:
                 activations(i + 1)
+            if i == 0:
+                scale_x(0)
+            for j in rows_at.get(i - 1, []):
+                store_row(0, j)
             if i - 1 in r_at:
                 add_r(r_at[i - 1])
                 empty_r(r_at[i - 1])
@@ -380,13 +394,17 @@ def tile_mopn_layer_pa_v_kernel(tc, x, norm_w, Wg, Wu, zg, zu, rstd, grad_out, o
             if not last:
                 move_go(i + 1)
             if i + 2 < STEPS:
-                load_rest(i + 2)
+                load_go(i + 2)
+                load_zu(i + 2)
+            if last:
+                for b in range(2, NBLK):
+                    matmul_dr(1, 0, b)
             gate_du(i)
             turn_du(i)
             empty_dz(i, 1)
             if 1 <= i <= 8:
                 turn_w(i - 1)
-            if i >= 2:
+            if i >= 2 and not last:
                 interleave(i // 2 - 1, i % 2)
             if i + 2 in r_at:
                 scale_x(r_at[i + 2])
@@ -400,69 +418,85 @@ def tile_mopn_layer_pa_v_kernel(tc, x, norm_w, Wg, Wu, zg, zu, rstd, grad_out, o
                 quantize_tok(i // 2 - 2)
             if i >= 3 and i % 2 == 1:
                 quantize_dz(i // 2 - 1, 0)
+            if last:
+                quantize_tok(6)
+            if i == 0:
+                nc.vector.tensor_scalar(out=rs_half[:], in0=rs[:], scalar1=0.5, scalar2=None, op0=ALU.mult)
+                nc.vector.scalar_tensor_tensor(out=rs_sq[:], in0=rs[:], scalar=-1.0 / D, in1=rs[:], op0=ALU.mult, op1=ALU.mult)
+            for key in grad_at.get(i, []):
+                weight_grad(*key)
             gate_slope(i)
+            gate_dg(i, nc.gpsimd)
             if i == 0:
                 fill_tables()
-            if last:
-                row_sums(0, PACK - 1)
-            gate_dg(i, nc.vector if i == 0 or last else nc.gpsimd)
             units = [lambda key=key: rotate_dr(*key) for key in dr_at.get(i, [])]
             if i in r_at:
                 r_prod[r_at[i]] = (work(), work())
                 units = [lambda h=h: rotate(r_prod[r_at[i]][h][:], x_banks[r_at[i]][h], r_at[i] % NBLK, 3 - 2 * h) for h in range(2)] + units
-            if rows and not last:
-                row_sums(0, rows[0])
+            for j in rows:
+                row_sums(0, j)
+            for unit in units[:-1]:
+                unit()
+            if not last:
                 gate_common(i + 1)
-            elif not last:
-                for unit in units[:-1]:
-                    unit()
-                gate_common(i + 1)
-                for unit in units[-1:]:
-                    unit()
             for j in rows:
                 join_sums(0, j)
+            for unit in units[-1:]:
+                unit()
+            for j in rows:
                 finish_row(0, j)
             feed(i + 1)
-            for key in grad_at.get(i, []):
-                weight_grad(*key)
-            for j in rows:
-                store_row(0, j)
+
+        def tail_scale(j):
+            res[1, j] = work()
+            for half in range(2):
+                nc.scalar.activation(out=res[1, j][:, half, :], in_=dn_banks[1, j][half][:], func=ACT.Copy, scale=rs_half[:, 1, j : j + 1])
+
+        def tail_sum(j):
+            spill = work()
+            nc.vector.scalar_tensor_tensor(
+                out=spill[:].rearrange("p s c -> p (s c)"), in0=res[1, j][:].rearrange("p s c -> p (s c)"), scalar=rs_sq[:, 1, j : j + 1],
+                in1=xs[1][:, j, :], op0=ALU.mult, op1=ALU.mult, accum_out=sums[:, PACK + j, 2:3],
+            )
+
+        def tail_finish(j, pieces):
+            row = res[1, j][:].rearrange("p s c -> p (s c)")
+            for k in range(pieces):
+                cols = slice(k * D // pieces, (k + 1) * D // pieces)
+                nc.vector.scalar_tensor_tensor(
+                    out=row[:, cols], in0=xs[1][:, j, cols], scalar=sums[:, PACK + j, 2:3], in1=row[:, cols], op0=ALU.mult, op1=ALU.add
+                )
+                nc.sync.dma_start(out=o0_v[1, :, j, cols], in_=row[:, cols])
 
         turn_dg(STEPS - 1)
         empty_dz(STEPS - 1, 0)
-        for b in range(2, NBLK):
-            matmul_dr(1, 0, b)
         for half in range(2):
             interleave(7, half)
-        quantize_tok(6)
+        rotate_dr(1, 0, 2)
+        quantize_dz(7, 1)
+        quantize_dz(7, 0)
+        rotate_dr(1, 0, 3)
+        quantize_tok(7)
         for b in range(NBLK):
-            if b == 2:
-                quantize_dz(7, 1)
-                quantize_dz(7, 0)
-            rotate_dr(1, 0, b)
-            if b < 2:
-                matmul_dr(1, 1, b, range(2))
-        for b in range(2):
-            matmul_dr(1, 1, b, range(2, 4))
-        for b in range(2, NBLK):
             matmul_dr(1, 1, b)
-        weight_grad(2, 0)
+        for j in range(2):
+            dn_banks[1, j] = (bank(), bank())
         for b in range(NBLK):
             rotate_dr(1, 1, b)
-        quantize_tok(7)
-        add_dn(1, 0)
-        add_dn(1, 1)
+            for j in range(2):
+                add_dn_block(1, j, b)
+        tail_scale(1)
+        for j in range(2, PACK):
+            weight_grad(3, j - 2)
+            add_dn(1, j)
+            tail_scale(j)
         row_sums(1, 0)
-        for j in range(PACK):
-            if j + 1 < PACK:
-                row_sums(1, j + 1)
-            join_sums(1, j)
-            finish_row(1, j)
-            if j + 2 < PACK:
-                add_dn(1, j + 2)
-            if j == 0:
-                weight_grad(2, 1)
-            if j == 1:
-                weight_grad(3, 0)
-                weight_grad(3, 1)
-            store_row(1, j, 2 if j == PACK - 1 else 1)
+        join_sums(1, 0)
+        tail_sum(1)
+        finish_row(1, 0)
+        store_row(1, 0)
+        tail_finish(1, 1)
+        tail_sum(2)
+        tail_sum(3)
+        tail_finish(2, 1)
+        tail_finish(3, 2)

@@ -8,6 +8,7 @@ B, S, NS, DS, H = 8, 128, 2, 512, 1024
 D = NS * DS
 T = B * S
 FLOPS = 2 * NS * T * DS * 2 * H + 2 * NS * T * DS * H
+ROPE_BASE = 10000.0
 
 F32 = mybir.dt.float32
 BF16 = mybir.dt.bfloat16
@@ -23,7 +24,15 @@ P = 128
 PACK = 4
 KP = P * PACK
 NBLK = DS // P
-STEPS = 16
+GROUPS = T // KP
+CHUNKS = GROUPS * NS * (H // KP)
+STEPS = 2 * CHUNKS
+W_TILES = 2 * NS * (H // KP)
+DG, DU = 0, 1
+
+SLOTS = 5
+DR_SLOT = (0, 2)
+X_SLOT = (3, 1)
 
 
 def tile_mopn_layer_pa_v_kernel(tc, x, norm_w, Wg, Wu, zg, zu, rstd, grad_out, out_0, out_1):
@@ -34,7 +43,7 @@ def tile_mopn_layer_pa_v_kernel(tc, x, norm_w, Wg, Wu, zg, zu, rstd, grad_out, o
     zu_v = zu.rearrange(by_token).rearrange(tokens, p=P, j=PACK)
     go_v = grad_out.rearrange(by_token).rearrange(tokens, p=P, j=PACK)
     x_v = x.rearrange("b s d -> (b s) d").rearrange(tokens, p=P, j=PACK)
-    o0_v = out_0.rearrange("b s d -> (b s) d").rearrange(tokens, p=P, j=PACK)
+    dx_v = out_0.rearrange("b s d -> (b s) d").rearrange(tokens, p=P, j=PACK)
     weights = (Wg, Wu)
 
     with ExitStack() as ctx:
@@ -60,33 +69,38 @@ def tile_mopn_layer_pa_v_kernel(tc, x, norm_w, Wg, Wu, zg, zu, rstd, grad_out, o
 
         ident = keep.tile([P, P], F32, name="ident")
         ident16 = keep.tile([P, P], BF16, name="ident16")
-        rs_half = keep.tile([P, 2, PACK], F32, name="rs_half")
-        rs = keep.tile([P, 2, PACK], F32, name="rs")
-        rs_sq = keep.tile([P, 2, PACK], F32, name="rs_sq")
-        tables = keep.tile([P, NBLK, 5, P], F32, name="tables")
-        sums = keep.tile([P, 2 * PACK, 8], F32, name="sums")
-        xs, zgs, zus, gos, ths, sil, dgs, dus = {}, {}, {}, {}, {}, {}, {}, {}
-        dzT, tok, raw_w, w_grp, w_q, dz_q, tok_q = {}, {}, {}, {}, {}, {}, {}
-        xhat, x_banks, r_prod, r_banks, r_grp, r_q = {}, {}, {}, {}, {}, {}
-        go_banks = {}
-        dr_banks, turned, dn_banks, res, dz_banks = {}, {}, {}, {}, {}
+        rs_half = keep.tile([P, GROUPS, PACK], F32, name="rs_half")
+        rs = keep.tile([P, GROUPS, PACK], F32, name="rs")
+        rs_sq = keep.tile([P, GROUPS, PACK], F32, name="rs_sq")
+        tables = keep.tile([P, NBLK, SLOTS, P], F32, name="tables")
+        sums = keep.tile([P, GROUPS * PACK, 8], F32, name="sums")
+
+        xs, zgs, zus, gos, go_banks = {}, {}, {}, {}, {}
+        common, slope, dgs, dus = {}, {}, {}, {}
+        dz_grouped, dz_q, tok_grouped, tok_q = {}, {}, {}, {}
+        raw_w, w_grouped, w_q = {}, {}, {}
+        xhat, x_banks, r_terms, r_banks, r_grouped, r_q = {}, {}, {}, {}, {}, {}
+        dr_banks, dn_terms, dn_banks, dx_rows = {}, {}, {}, {}
 
         def place(i):
-            c, jp = divmod(i, 2)
-            return c // 4, slice(c % 4 * KP, (c % 4 + 1) * KP), slice(2 * jp, 2 * jp + 2)
+            c, pair = divmod(i, 2)
+            return c // 4, slice(2 * pair, 2 * pair + 2), slice(c % 4 * KP, (c % 4 + 1) * KP)
+
+        def zg_tile():
+            return flow.tile([P, 2, KP], F32, name="zg", tag="zg", bufs=3)
 
         def load_zg(i):
-            g, cols, js = place(i)
-            zgs[i] = flow.tile([P, 2, KP], F32, name="zg", tag="zg", bufs=3)
+            g, js, cols = place(i)
+            zgs[i] = zg_tile()
             nc.sync.dma_start(out=zgs[i][:], in_=zg_v[g, :, js, cols])
 
         def load_go(i):
-            g, cols, js = place(i)
-            gos[i] = flow.tile([P, 2, KP], BF16, name="go", tag="go", bufs=2)
+            g, js, cols = place(i)
+            gos[i] = flow.tile([P, 2, KP], BF16, name="go", tag="go")
             nc.sync.dma_start(out=gos[i][:], in_=go_v[g, :, js, cols])
 
         def load_zu(i):
-            g, cols, js = place(i)
+            g, js, cols = place(i)
             zus[i] = flow.tile([P, 2, KP], F32, name="zu", tag="zu", bufs=3)
             nc.sync.dma_start(out=zus[i][:], in_=zu_v[g, :, js, cols])
 
@@ -95,85 +109,79 @@ def tile_mopn_layer_pa_v_kernel(tc, x, norm_w, Wg, Wu, zg, zu, rstd, grad_out, o
             nc.sync.dma_start(out=xs[g][:], in_=x_v[g])
 
         def load_w(k):
-            n, which, h2 = k // 4, k % 2, k % 4 // 2
+            n, h, which = k // 4, k % 4 // 2, k % 2
             raw_w[k] = flow.tile([P, NBLK, KP], BF16, name="raw_w", tag="raw_w")
-            rows = weights[which][n].rearrange("(b p) h -> p b h", p=P)
-            nc.sync.dma_start(out=raw_w[k][:], in_=rows[:, :, h2 * KP : (h2 + 1) * KP])
+            w_by_block = weights[which][n].rearrange("(b p) f -> p b f", p=P)
+            nc.sync.dma_start(out=raw_w[k][:], in_=w_by_block[:, :, h * KP : (h + 1) * KP])
 
-        def turn_words(src, rows):
+        def turn_words(src, first):
             dst = bank()
             view = dst[:].rearrange("p (u r m) -> p u r m", u=2, r=2)
             words = src[:].bitcast(F32)
             for u in range(2):
                 for r in range(2):
-                    nc.tensor.transpose(view[:, u, r, :], words[:, rows + r, u : 2 * P : 2], ident[:])
+                    nc.tensor.transpose(view[:, u, r, :], words[:, first + r, u : 2 * P : 2], ident[:])
             return dst
 
         def empty_words(dst, half, src):
             out = dst[:].bitcast(F32).rearrange("p (h m u) -> p h m u", h=2, u=2)[:, half]
             nc.scalar.copy(out=out, in_=src[:].rearrange("p (u m) -> p m u", u=2))
 
+        def turn_w(k):
+            w_grouped[k] = grouped()
+            for half in range(2):
+                empty_words(w_grouped[k], half, turn_words(raw_w[k], 2 * half))
+
+        def quantize_w(k):
+            w_q[k] = quantize(w_grouped[k], E4, "w_q", W_TILES)
+
         def activations(i):
-            ths[i], sil[i] = work(), work()
-            nc.scalar.activation(out=ths[i][:], in_=zgs[i][:], func=ACT.Tanh, scale=-0.5)
-            nc.scalar.activation(out=sil[i][:], in_=zgs[i][:], func=ACT.Silu, scale=-1.0)
+            common[i], slope[i] = work(), work()
+            nc.scalar.activation(out=common[i][:], in_=zgs[i][:], func=ACT.Tanh, scale=-0.5)
+            nc.scalar.activation(out=slope[i][:], in_=zgs[i][:], func=ACT.Silu, scale=-1.0)
 
         def move_go(i):
             go_banks[i] = psum.tile([P, 2, KP], BF16, name="bank", tag="bank")
             for r in range(2):
                 nc.tensor.matmul(go_banks[i][:, r, :], lhsT=ident16[:], rhs=gos[i][:, r, :], start=True, stop=True)
 
-        def gate_common(i, js=slice(0, 2)):
-            src = go_banks[i] if i in go_banks else gos[i]
-            nc.vector.scalar_tensor_tensor(out=ths[i][:, js], in0=ths[i][:, js], scalar=1.0, in1=src[:, js], op0=ALU.subtract, op1=ALU.mult)
+        def gate_common(dst, go):
+            nc.vector.scalar_tensor_tensor(out=dst, in0=dst, scalar=1.0, in1=go, op0=ALU.subtract, op1=ALU.mult)
 
         def gate_du(i):
             dus[i] = flow.tile([P, 2, KP], BF16, name="du", tag="du")
-            nc.vector.scalar_tensor_tensor(out=dus[i][:], in0=ths[i][:], scalar=-1.0, in1=zgs[i][:], op0=ALU.mult, op1=ALU.mult)
+            nc.vector.scalar_tensor_tensor(out=dus[i][:], in0=common[i][:], scalar=-1.0, in1=zgs[i][:], op0=ALU.mult, op1=ALU.mult)
 
         def gate_slope(i):
-            nc.vector.scalar_tensor_tensor(out=sil[i][:], in0=sil[i][:], scalar=1.0, in1=zus[i][:], op0=ALU.subtract, op1=ALU.mult)
+            nc.vector.scalar_tensor_tensor(out=slope[i][:], in0=slope[i][:], scalar=1.0, in1=zus[i][:], op0=ALU.subtract, op1=ALU.mult)
 
-        def gate_dg(i, engine):
-            c, jp = divmod(i, 2)
-            if jp == 0:
+        def gate_dg(i):
+            c, pair = divmod(i, 2)
+            if pair == 0:
                 dgs[c] = flow.tile([P, PACK, KP], BF16, name="dg", tag="dg")
-            engine.tensor_tensor(out=dgs[c][:, 2 * jp : 2 * jp + 2, :], in0=ths[i][:], in1=sil[i][:], op=ALU.mult)
+            nc.gpsimd.tensor_tensor(out=dgs[c][:, 2 * pair : 2 * pair + 2, :], in0=common[i][:], in1=slope[i][:], op=ALU.mult)
 
-        def turn_du(i):
-            dz_banks[i, 1] = turn_words(dus[i], 0)
+        def turn_dz(i, which):
+            c, pair = divmod(i, 2)
+            src = turn_words(dgs[c], 2 * pair) if which == DG else turn_words(dus[i], 0)
+            if pair == 0:
+                dz_grouped[c, which] = grouped()
+            empty_words(dz_grouped[c, which], pair, src)
 
-        def turn_dg(i):
-            dz_banks[i, 0] = turn_words(dgs[i // 2], 2 * (i % 2))
-
-        def empty_dz(i, which):
-            c, jp = divmod(i, 2)
-            if jp == 0:
-                dzT[c, which] = grouped()
-            empty_words(dzT[c, which], jp, dz_banks[i, which])
+        def quantize_dz(c, which):
+            dz_q[c, which] = quantize(dz_grouped[c, which], E5, "dz_q", 6)
 
         def interleave(c, half):
             if half == 0:
-                tok[c] = grouped()
-            cols = slice(half * 64, (half + 1) * 64)
+                tok_grouped[c] = grouped()
+            quads = slice(half * KP // 8, (half + 1) * KP // 8)
             nc.scalar.copy(
-                out=tok[c][:].rearrange("p (c i j) -> p c j i", i=4, j=PACK)[:, cols],
-                in_=dgs[c][:].rearrange("p j (c i) -> p c j i", i=4)[:, cols],
+                out=tok_grouped[c][:].rearrange("p (q f j) -> p q j f", f=4, j=PACK)[:, quads],
+                in_=dgs[c][:].rearrange("p j (q f) -> p q j f", f=4)[:, quads],
             )
 
-        def quantize_dz(c, which):
-            dz_q[c, which] = quantize(dzT[c, which], E5, "dz_q", 6)
-
         def quantize_tok(c):
-            tok_q[c] = quantize(tok[c], E5, "tok_q", 6)
-
-        def turn_w(k):
-            w_grp[k] = grouped()
-            for half in range(2):
-                empty_words(w_grp[k], half, turn_words(raw_w[k], 2 * half))
-
-        def quantize_w(k):
-            w_q[k] = quantize(w_grp[k], E4, "w_q", 8)
+            tok_q[c] = quantize(tok_grouped[c], E5, "tok_q", 6)
 
         def rotate(out, src, b, slot):
             shape = [P, 2, PACK, 4, 32]
@@ -190,36 +198,32 @@ def tile_mopn_layer_pa_v_kernel(tc, x, norm_w, Wg, Wu, zg, zu, rstd, grad_out, o
 
         def scale_x(u):
             g, b = divmod(u, NBLK)
-            xhat[u] = work()
-            dst = xhat[u][:].rearrange("p s (a c) -> p (s a) c", c=2 * P).rearrange("p j (h c) -> p j h c", h=2)
+            xhat[u] = work()[:].rearrange("p s (a c) -> p (s a) c", c=2 * P)
+            dst = xhat[u].rearrange("p j (h c) -> p j h c", h=2)
             src = xs[g][:].rearrange("p j (h b c) -> p j h b c", h=2, c=P)
             for j in range(PACK):
                 nc.scalar.activation(out=dst[:, j], in_=src[:, j, :, b, :], func=ACT.Copy, scale=rs[:, g, j : j + 1])
 
         def turn_x(u):
-            src = xhat[u][:].rearrange("p s (a c) -> p (s a) c", c=2 * P)
             x_banks[u] = (bank(), bank())
             for half in range(2):
                 for j in range(PACK):
-                    nc.tensor.transpose(x_banks[u][half][:, j * P : (j + 1) * P], src[:, j, half * P : (half + 1) * P], ident[:])
+                    nc.tensor.transpose(x_banks[u][half][:, j * P : (j + 1) * P], xhat[u][:, j, half * P : (half + 1) * P], ident[:])
 
-        def rotate_x(u):
-            r_prod[u] = (work(), work())
-            rotate(r_prod[u][0][:], x_banks[u][0], u % NBLK, 3)
-            rotate(r_prod[u][1][:], x_banks[u][1], u % NBLK, 1)
+        def rotate_x(u, half):
+            r_terms[u, half] = work()
+            rotate(r_terms[u, half][:], x_banks[u][half], u % NBLK, X_SLOT[half])
 
         def add_r(u):
             r_banks[u] = (bank(), bank())
             for half in range(2):
                 for j in range(PACK):
                     cols = slice(j * P, (j + 1) * P)
-                    add_turned(r_banks[u][half][:, cols], r_prod[u][0][:, 1 - half, cols], r_prod[u][1][:, half, cols])
-
-        def empty_r(u):
-            r_grp[u] = flow.tile([P, 2, KP], BF16, name="r_grp", tag="r_grp", align_bytes=64)
+                    add_turned(r_banks[u][half][:, cols], r_terms[u, 0][:, 1 - half, cols], r_terms[u, 1][:, half, cols])
+            r_grouped[u] = flow.tile([P, 2, KP], BF16, name="r_grouped", tag="r_grouped", align_bytes=64)
             for half in range(2):
                 nc.scalar.copy(
-                    out=r_grp[u][:, half, :].rearrange("p (c j) -> p c j", j=PACK),
+                    out=r_grouped[u][:, half, :].rearrange("p (c j) -> p c j", j=PACK),
                     in_=r_banks[u][half][:].rearrange("p (j c) -> p c j", j=PACK),
                 )
 
@@ -231,7 +235,7 @@ def tile_mopn_layer_pa_v_kernel(tc, x, norm_w, Wg, Wu, zg, zu, rstd, grad_out, o
                 r_q[g] = (codes, scales)
             cols = slice(2 * b * P, 2 * (b + 1) * P)
             nc.vector.quantize_mx(
-                out=r_q[g][0][:, cols].bitcast(E4), scales=r_q[g][1][:, cols], in_=r_grp[u][:].rearrange("p s c -> p (s c)")
+                out=r_q[g][0][:, cols].bitcast(E4), scales=r_q[g][1][:, cols], in_=r_grouped[u][:].rearrange("p s c -> p (s c)")
             )
 
         def mx(acc, lhs, cols, rhs, start, stop):
@@ -240,77 +244,102 @@ def tile_mopn_layer_pa_v_kernel(tc, x, norm_w, Wg, Wu, zg, zu, rstd, grad_out, o
                 rhs=rhs[0][:].bitcast(E5), rhs_scale=rhs[1][:], start=start, stop=stop,
             )
 
-        def matmul_dr(g, n, b, passes=range(4)):
-            if 0 in passes:
-                dr_banks[g, n, b] = bank()
-            for k in passes:
-                mx(dr_banks[g, n, b], w_q[4 * n + k], slice(b * P, (b + 1) * P), dz_q[4 * g + 2 * n + k // 2, k % 2], k == 0, k == 3)
+        def matmul_dr(g, n, b):
+            dr_banks[g, n, b] = bank()
+            for k in range(4):
+                h, which = divmod(k, 2)
+                mx(dr_banks[g, n, b], w_q[4 * n + k], slice(b * P, (b + 1) * P), dz_q[4 * g + 2 * n + h, which], k == 0, k == 3)
+
+        def weight_grad(c, pair):
+            n, h = divmod(c, 2)
+            stage = work()
+            for s in range(2):
+                b = 2 * pair + s
+                acc = bank()
+                for g in range(GROUPS):
+                    mx(acc, r_q[g], slice((2 * b + n) * P, (2 * b + n + 1) * P), tok_q[4 * g + c], g == 0, g == GROUPS - 1)
+                nc.scalar.activation(out=stage[:, s, :], in_=acc[:], func=ACT.Copy, scale=0.5)
+            dw_by_block = out_1[n].rearrange("(b p) f -> p b f", p=P)
+            nc.sync.dma_start(out=dw_by_block[:, 2 * pair : 2 * pair + 2, h * KP : (h + 1) * KP], in_=stage[:])
 
         def rotate_dr(g, n, b):
             if b == 0:
-                turned[g, n] = flow.tile([P, NBLK, 2, KP], F32, name="turned", tag="turned")
-            rotate(turned[g, n][:, b], dr_banks[g, n, b], b, 2 * n)
+                dn_terms[g, n] = flow.tile([P, NBLK, 2, KP], F32, name="dn_terms", tag="dn_terms")
+            rotate(dn_terms[g, n][:, b], dr_banks[g, n, b], b, DR_SLOT[n])
 
         def add_dn_block(g, j, b):
             cols = slice(j * P, (j + 1) * P)
             for half in range(2):
-                add_turned(dn_banks[g, j][half][:, b * P : (b + 1) * P], turned[g, 0][:, b, half, cols], turned[g, 1][:, b, 1 - half, cols])
+                dst = dn_banks[g, j][half][:, b * P : (b + 1) * P]
+                add_turned(dst, dn_terms[g, 0][:, b, half, cols], dn_terms[g, 1][:, b, 1 - half, cols])
 
         def add_dn(g, j):
             dn_banks[g, j] = (bank(), bank())
             for b in range(NBLK):
                 add_dn_block(g, j, b)
 
+        def total(g, j):
+            return sums[:, PACK * g + j, 2:3]
+
         def row_sums(g, j):
-            res[g, j] = work()
+            dx_rows[g, j] = work()
             for half in range(2):
                 nc.vector.scalar_tensor_tensor(
-                    out=res[g, j][:, half, :], in0=dn_banks[g, j][half][:], scalar=rs_sq[:, g, j : j + 1],
+                    out=dx_rows[g, j][:, half, :], in0=dn_banks[g, j][half][:], scalar=rs_sq[:, g, j : j + 1],
                     in1=xs[g][:, j, half * DS : (half + 1) * DS], op0=ALU.mult, op1=ALU.mult,
                     accum_out=sums[:, PACK * g + j, half : half + 1],
                 )
 
         def join_sums(g, j):
-            row = sums[:, PACK * g + j, :]
-            nc.vector.tensor_scalar(out=row[:, 2:3], in0=row[:, 0:1], scalar1=row[:, 1:2], scalar2=None, op0=ALU.add)
+            halves = sums[:, PACK * g + j, :]
+            nc.vector.tensor_scalar(out=total(g, j), in0=halves[:, 0:1], scalar1=halves[:, 1:2], scalar2=None, op0=ALU.add)
 
         def finish_row(g, j):
             for half in range(2):
                 nc.vector.scalar_tensor_tensor(
-                    out=res[g, j][:, half, :], in0=xs[g][:, j, half * DS : (half + 1) * DS], scalar=sums[:, PACK * g + j, 2:3],
+                    out=dx_rows[g, j][:, half, :], in0=xs[g][:, j, half * DS : (half + 1) * DS], scalar=total(g, j),
                     in1=dn_banks[g, j][half][:], op0=ALU.mult, op1=ALU.add,
                 )
 
-        def store_row(g, j, pieces=1):
-            row = res[g, j][:].rearrange("p s c -> p (s c)")
+        def store_row(g, j):
+            row = dx_rows[g, j][:].rearrange("p s c -> p (s c)")
+            nc.scalar.activation(out=row, in_=row, func=ACT.Copy, scale=rs_half[:, g, j : j + 1])
+            nc.sync.dma_start(out=dx_v[g, :, j, :], in_=row)
+
+        def scale_row(g, j):
+            dx_rows[g, j] = work()
+            for half in range(2):
+                nc.scalar.activation(
+                    out=dx_rows[g, j][:, half, :], in_=dn_banks[g, j][half][:], func=ACT.Copy, scale=rs_half[:, g, j : j + 1]
+                )
+
+        def scaled_row_sum(g, j):
+            products = work()
+            nc.vector.scalar_tensor_tensor(
+                out=products[:].rearrange("p s c -> p (s c)"), in0=dx_rows[g, j][:].rearrange("p s c -> p (s c)"),
+                scalar=rs_sq[:, g, j : j + 1], in1=xs[g][:, j, :], op0=ALU.mult, op1=ALU.mult, accum_out=total(g, j),
+            )
+
+        def finish_scaled_row(g, j, pieces):
+            row = dx_rows[g, j][:].rearrange("p s c -> p (s c)")
             for k in range(pieces):
                 cols = slice(k * D // pieces, (k + 1) * D // pieces)
-                nc.scalar.activation(out=row[:, cols], in_=row[:, cols], func=ACT.Copy, scale=rs_half[:, g, j : j + 1])
-                nc.sync.dma_start(out=o0_v[g, :, j, cols], in_=row[:, cols])
-
-        def weight_grad(c, pair):
-            n, h2 = divmod(c, 2)
-            stage = work()
-            for s in range(2):
-                b = 2 * pair + s
-                acc = bank()
-                for g in range(2):
-                    mx(acc, r_q[g], slice((2 * b + n) * P, (2 * b + n + 1) * P), tok_q[4 * g + c], g == 0, g == 1)
-                nc.scalar.activation(out=stage[:, s, :], in_=acc[:], func=ACT.Copy, scale=0.5)
-            rows = out_1[n].rearrange("(b p) h -> p b h", p=P)
-            nc.sync.dma_start(out=rows[:, 2 * pair : 2 * pair + 2, h2 * KP : (h2 + 1) * KP], in_=stage[:])
+                nc.vector.scalar_tensor_tensor(
+                    out=row[:, cols], in0=xs[g][:, j, cols], scalar=total(g, j), in1=row[:, cols], op0=ALU.mult, op1=ALU.add
+                )
+                nc.sync.dma_start(out=dx_v[g, :, j, cols], in_=row[:, cols])
 
         w_rows = keep.tile([P, P], BF16, name="w_rows")
         small = work()
         freq_row, w_rows32, pos = small[:, 0, 0:P], small[:, 0, P : 2 * P], small[:, 0, 2 * P : 3 * P]
         freq_col = keep.tile([P, 1], F32, name="freq_col")
         nc.vector.memset(w_rows[:], 0.0)
-        nc.vector.memset(freq_row, 1.0)
-        zgs[0] = flow.tile([P, 2, KP], F32, name="zg", tag="zg", bufs=3)
+        nc.vector.memset(freq_row[:, 0:1], 1.0)
+        zgs[0] = zg_tile()
         nc.sync.dma_start(out=zgs[0][:, 0, :], in_=zg_v[0, :, 0, 0:KP])
         load_go(0)
         nc.sync.dma_start(out=zgs[0][:, 1, :], in_=zg_v[0, :, 1, 0:KP])
-        nc.sync.dma_start(out=w_rows[0:8, :], in_=norm_w.rearrange("(c p) -> c p", p=P))
+        nc.sync.dma_start(out=w_rows[0 : D // P, :], in_=norm_w.rearrange("(c p) -> c p", p=P))
         load_zu(0)
         nc.sync.dma_start(out=rs[:], in_=rstd.rearrange("b s -> (b s)").rearrange("(g p j) -> p g j", p=P, j=PACK))
         load_zg(1)
@@ -320,27 +349,31 @@ def tile_mopn_layer_pa_v_kernel(tc, x, norm_w, Wg, Wu, zg, zu, rstd, grad_out, o
         nc.gpsimd.iota(pos, pattern=[[1, PACK], [PACK, 32]], base=0, channel_multiplier=0, allow_small_or_imprecise_dtypes=True)
         make_identity(nc, ident[:])
         nc.gpsimd.tensor_copy(out=ident16[:], in_=ident[:])
-        step = math.log(10000.0) / DS
+        decay = math.log(ROPE_BASE) / DS
         for k in range(7):
-            w = 2**k
-            nc.vector.tensor_scalar(out=freq_row[:, w : 2 * w], in0=freq_row[:, 0:w], scalar1=math.exp(-step * w), scalar2=None, op0=ALU.mult)
+            filled = 2**k
+            nc.vector.tensor_scalar(
+                out=freq_row[:, filled : 2 * filled], in0=freq_row[:, 0:filled], scalar1=math.exp(-decay * filled), scalar2=None, op0=ALU.mult
+            )
         freq_bank, w_bank = bank(), bank()
         nc.tensor.transpose(freq_bank[:, 0:P], freq_row, ident[:])
         nc.vector.tensor_copy(out=freq_col[:], in_=freq_bank[:, 0:1])
-        ths[0], sil[0] = work(), work()
-        for func, scale, dst, r in ((ACT.Silu, -1.0, sil, 0), (ACT.Tanh, -0.5, ths, 0), (ACT.Tanh, -0.5, ths, 1), (ACT.Silu, -1.0, sil, 1)):
-            nc.scalar.activation(out=dst[0][:, r, :], in_=zgs[0][:, r, :], func=func, scale=scale)
+        common[0], slope[0] = work(), work()
+        for func, scale, dst, r in (
+            (ACT.Silu, -1.0, slope[0], 0), (ACT.Tanh, -0.5, common[0], 0), (ACT.Tanh, -0.5, common[0], 1), (ACT.Silu, -1.0, slope[0], 1)
+        ):
+            nc.scalar.activation(out=dst[:, r, :], in_=zgs[0][:, r, :], func=func, scale=scale)
         trig = work()
         turns, whole = trig[:, 0, :], trig[:, 1, :].bitcast(I32)
         for b in range(NBLK):
             nc.vector.tensor_scalar(
                 out=turns[:, b * P : (b + 1) * P], in0=pos, scalar1=freq_col[:],
-                scalar2=math.exp(-step * P * b) / (2 * math.pi), op0=ALU.mult, op1=ALU.mult,
+                scalar2=math.exp(-decay * P * b) / (2 * math.pi), op0=ALU.mult, op1=ALU.mult,
             )
         nc.vector.tensor_copy(out=whole, in_=turns)
-        gate_common(0, slice(0, 1))
+        gate_common(common[0][:, 0:1], gos[0][:, 0:1])
         nc.vector.tensor_tensor(out=turns, in0=turns, in1=whole, op=ALU.subtract)
-        gate_common(0, slice(1, 2))
+        gate_common(common[0][:, 1:2], gos[0][:, 1:2])
         nc.vector.tensor_copy(out=w_rows32, in_=w_rows[:])
         nc.tensor.transpose(w_bank[:, 0:P], w_rows32, ident[:])
         sin, cos = small[:, 1, :], trig[:, 1, :]
@@ -349,154 +382,130 @@ def tile_mopn_layer_pa_v_kernel(tc, x, norm_w, Wg, Wu, zg, zu, rstd, grad_out, o
         nc.scalar.activation(out=cos, in_=cos, func=ACT.Sin, scale=-2 * math.pi, bias=math.pi / 2)
 
         def fill_tables():
-            for slot, (wave, sign, half) in enumerate(((sin, -1.0, 1), (sin, 1.0, 0), (cos, 1.0, 0), (cos, 1.0, 1), (cos, 1.0, 0))):
+            for slot, wave, sign, half in ((1, sin, -1.0, 1), (3, sin, 1.0, 0), (0, cos, 1.0, 0), (2, cos, 1.0, 1), (4, cos, 1.0, 0)):
                 gain = w_bank[:, NBLK * half : NBLK * (half + 1)].rearrange("p (b a) -> p b a", a=1).to_broadcast([P, NBLK, P])
                 nc.vector.scalar_tensor_tensor(
-                    out=tables[:, :, (1, 3, 0, 2, 4)[slot], :], in0=wave.rearrange("p (b c) -> p b c", c=P), scalar=sign, in1=gain, op0=ALU.mult, op1=ALU.mult
+                    out=tables[:, :, slot, :], in0=wave.rearrange("p (b c) -> p b c", c=P), scalar=sign, in1=gain, op0=ALU.mult, op1=ALU.mult
                 )
 
-        r_at = {1: 0, 2: 1, 3: 2, 4: 3, 5: 4, 8: 5, 9: 6, 11: 7}
         dr_at = {6: [(0, 0, 0), (0, 0, 1)], 7: [(0, 0, 2), (0, 0, 3)], 10: [(0, 1, b) for b in range(NBLK)], 15: [(1, 0, 0), (1, 0, 1)]}
-        rows_at = {11: [0], 12: [1], 13: [2], 14: [3]}
-        grad_at = {13: [(0, 0), (0, 1)], 14: [(1, 0), (1, 1)], 15: [(2, 0), (2, 1)]}
+        row_at = {11 + j: j for j in range(PACK)}
+        r_at = {i: u for u, i in enumerate([i for i in range(1, STEPS) if i not in dr_at][: GROUPS * NBLK])}
+        grad_at = {13: 0, 14: 1}
 
         def feed(i):
             if i in r_at:
                 turn_x(r_at[i])
             for key in dr_at.get(i, []):
                 matmul_dr(*key)
-            for j in rows_at.get(i, []):
-                add_dn(0, j)
+            if i in row_at:
+                add_dn(0, row_at[i])
 
         for i in range(STEPS):
             last = i == STEPS - 1
-            rows = rows_at.get(i, [])
+            c, pair = divmod(i, 2)
             if i + 2 < STEPS:
                 load_zg(i + 2)
-            if i < 8:
+            if i < W_TILES:
                 load_w(i)
             if i == 2:
                 load_x(1)
-            if last:
-                interleave(6, 1)
-            else:
+            if not last:
                 activations(i + 1)
             if i == 0:
                 scale_x(0)
-            for j in rows_at.get(i - 1, []):
-                store_row(0, j)
-            if i - 1 in r_at:
-                add_r(r_at[i - 1])
-                empty_r(r_at[i - 1])
-            if i >= 1:
-                turn_dg(i - 1)
-                empty_dz(i - 1, 0)
             if not last:
                 move_go(i + 1)
             if i + 2 < STEPS:
                 load_go(i + 2)
                 load_zu(i + 2)
+            if i - 1 in row_at:
+                store_row(0, row_at[i - 1])
+            if i - 1 in r_at:
+                add_r(r_at[i - 1])
+            if i >= 1:
+                turn_dz(i - 1, DG)
             if last:
                 for b in range(2, NBLK):
                     matmul_dr(1, 0, b)
-            gate_du(i)
-            turn_du(i)
-            empty_dz(i, 1)
-            if 1 <= i <= 8:
+            if 1 <= i <= W_TILES:
                 turn_w(i - 1)
-            if i >= 2 and not last:
-                interleave(i // 2 - 1, i % 2)
+            gate_du(i)
+            turn_dz(i, DU)
+            if c >= 1:
+                interleave(c - 1, pair)
             if i + 2 in r_at:
                 scale_x(r_at[i + 2])
-            if 2 <= i <= 9:
-                quantize_w(i - 2)
             if i - 2 in r_at:
                 quantize_r(r_at[i - 2])
-            if i >= 2 and i % 2 == 0:
-                quantize_dz(i // 2 - 1, 1)
-            if i >= 4 and i % 2 == 0:
-                quantize_tok(i // 2 - 2)
-            if i >= 3 and i % 2 == 1:
-                quantize_dz(i // 2 - 1, 0)
-            if last:
-                quantize_tok(6)
+            if c >= 1 and pair == 1:
+                quantize_dz(c - 1, DG)
+            if 2 <= i < W_TILES + 2:
+                quantize_w(i - 2)
+            if c >= 1 and pair == 0:
+                quantize_dz(c - 1, DU)
+            if c >= 2 and pair == 0:
+                quantize_tok(c - 2)
             if i == 0:
                 nc.vector.tensor_scalar(out=rs_half[:], in0=rs[:], scalar1=0.5, scalar2=None, op0=ALU.mult)
                 nc.vector.scalar_tensor_tensor(out=rs_sq[:], in0=rs[:], scalar=-1.0 / D, in1=rs[:], op0=ALU.mult, op1=ALU.mult)
-            for key in grad_at.get(i, []):
-                weight_grad(*key)
+            if i in grad_at:
+                for block_pair in range(2):
+                    weight_grad(grad_at[i], block_pair)
             gate_slope(i)
-            gate_dg(i, nc.gpsimd)
+            gate_dg(i)
             if i == 0:
                 fill_tables()
-            units = [lambda key=key: rotate_dr(*key) for key in dr_at.get(i, [])]
-            if i in r_at:
-                r_prod[r_at[i]] = (work(), work())
-                units = [lambda h=h: rotate(r_prod[r_at[i]][h][:], x_banks[r_at[i]][h], r_at[i] % NBLK, 3 - 2 * h) for h in range(2)] + units
-            for j in rows:
-                row_sums(0, j)
-            for unit in units[:-1]:
-                unit()
+            rotations = [(rotate_x, (r_at[i], half)) for half in range(2)] if i in r_at else []
+            rotations = rotations + [(rotate_dr, key) for key in dr_at.get(i, [])]
+            if i in row_at:
+                row_sums(0, row_at[i])
+            for func, key in rotations[:-1]:
+                func(*key)
             if not last:
-                gate_common(i + 1)
-            for j in rows:
-                join_sums(0, j)
-            for unit in units[-1:]:
-                unit()
-            for j in rows:
-                finish_row(0, j)
+                gate_common(common[i + 1][:], go_banks[i + 1][:])
+            if i in row_at:
+                join_sums(0, row_at[i])
+            for func, key in rotations[-1:]:
+                func(*key)
+            if i in row_at:
+                finish_row(0, row_at[i])
             feed(i + 1)
 
-        def tail_scale(j):
-            res[1, j] = work()
-            for half in range(2):
-                nc.scalar.activation(out=res[1, j][:, half, :], in_=dn_banks[1, j][half][:], func=ACT.Copy, scale=rs_half[:, 1, j : j + 1])
-
-        def tail_sum(j):
-            spill = work()
-            nc.vector.scalar_tensor_tensor(
-                out=spill[:].rearrange("p s c -> p (s c)"), in0=res[1, j][:].rearrange("p s c -> p (s c)"), scalar=rs_sq[:, 1, j : j + 1],
-                in1=xs[1][:, j, :], op0=ALU.mult, op1=ALU.mult, accum_out=sums[:, PACK + j, 2:3],
-            )
-
-        def tail_finish(j, pieces):
-            row = res[1, j][:].rearrange("p s c -> p (s c)")
-            for k in range(pieces):
-                cols = slice(k * D // pieces, (k + 1) * D // pieces)
-                nc.vector.scalar_tensor_tensor(
-                    out=row[:, cols], in0=xs[1][:, j, cols], scalar=sums[:, PACK + j, 2:3], in1=row[:, cols], op0=ALU.mult, op1=ALU.add
-                )
-                nc.sync.dma_start(out=o0_v[1, :, j, cols], in_=row[:, cols])
-
-        turn_dg(STEPS - 1)
-        empty_dz(STEPS - 1, 0)
+        turn_dz(STEPS - 1, DG)
         for half in range(2):
-            interleave(7, half)
+            interleave(CHUNKS - 1, half)
         rotate_dr(1, 0, 2)
-        quantize_dz(7, 1)
-        quantize_dz(7, 0)
+        quantize_tok(CHUNKS - 2)
+        quantize_dz(CHUNKS - 1, DU)
+        for block_pair in range(2):
+            weight_grad(2, block_pair)
+        quantize_dz(CHUNKS - 1, DG)
         rotate_dr(1, 0, 3)
-        quantize_tok(7)
         for b in range(NBLK):
             matmul_dr(1, 1, b)
         for j in range(2):
             dn_banks[1, j] = (bank(), bank())
         for b in range(NBLK):
             rotate_dr(1, 1, b)
+            if b == 0:
+                quantize_tok(CHUNKS - 1)
             for j in range(2):
                 add_dn_block(1, j, b)
-        tail_scale(1)
-        for j in range(2, PACK):
-            weight_grad(3, j - 2)
-            add_dn(1, j)
-            tail_scale(j)
+        scale_row(1, 1)
+        weight_grad(3, 0)
+        add_dn(1, 2)
+        add_dn(1, 3)
         row_sums(1, 0)
         join_sums(1, 0)
-        tail_sum(1)
+        scaled_row_sum(1, 1)
         finish_row(1, 0)
+        scale_row(1, 2)
         store_row(1, 0)
-        tail_finish(1, 1)
-        tail_sum(2)
-        tail_sum(3)
-        tail_finish(2, 1)
-        tail_finish(3, 2)
+        scale_row(1, 3)
+        finish_scaled_row(1, 1, 1)
+        weight_grad(3, 1)
+        scaled_row_sum(1, 2)
+        scaled_row_sum(1, 3)
+        finish_scaled_row(1, 2, 1)
+        finish_scaled_row(1, 3, 2)

@@ -244,11 +244,15 @@ def tile_mopn_layer_pa_v_kernel(tc, x, norm_w, Wg, Wu, zg, zu, rstd, grad_out, o
                 rhs=rhs[0][:].bitcast(E5), rhs_scale=rhs[1][:], start=start, stop=stop,
             )
 
-        def matmul_dr(g, n, b):
-            dr_banks[g, n, b] = bank()
-            for k in range(4):
-                h, which = divmod(k, 2)
-                mx(dr_banks[g, n, b], w_q[4 * n + k], slice(b * P, (b + 1) * P), dz_q[4 * g + 2 * n + h, which], k == 0, k == 3)
+        def matmul_dr(g, n, b, halves=(0, 1)):
+            if 0 in halves:
+                dr_banks[g, n, b] = bank()
+            for h in halves:
+                for which in (DU, DG):
+                    mx(
+                        dr_banks[g, n, b], w_q[4 * n + 2 * h + which], slice(b * P, (b + 1) * P), dz_q[4 * g + 2 * n + h, which],
+                        (h, which) == (0, DU), (h, which) == (1, DG),
+                    )
 
         def weight_grad(c, pair):
             n, h = divmod(c, 2)
@@ -462,28 +466,32 @@ def tile_mopn_layer_pa_v_kernel(tc, x, norm_w, Wg, Wu, zg, zu, rstd, grad_out, o
                 row_sums(0, row_at[i])
             for func, key in rotations[:-1]:
                 func(*key)
-            if not last:
-                gate_common(common[i + 1][:], go_banks[i + 1][:])
             if i in row_at:
+                gate_common(common[i + 1][:, 0:1], go_banks[i + 1][:, 0:1])
                 join_sums(0, row_at[i])
+                gate_common(common[i + 1][:, 1:2], go_banks[i + 1][:, 1:2])
+            elif not last:
+                gate_common(common[i + 1][:], go_banks[i + 1][:])
             for func, key in rotations[-1:]:
                 func(*key)
             if i in row_at:
                 finish_row(0, row_at[i])
             feed(i + 1)
 
+        for b in range(NBLK):
+            matmul_dr(1, 1, b, (0,))
         turn_dz(STEPS - 1, DG)
         for half in range(2):
             interleave(CHUNKS - 1, half)
         rotate_dr(1, 0, 2)
         quantize_tok(CHUNKS - 2)
         quantize_dz(CHUNKS - 1, DU)
-        for block_pair in range(2):
-            weight_grad(2, block_pair)
         quantize_dz(CHUNKS - 1, DG)
         rotate_dr(1, 0, 3)
+        weight_grad(2, 0)
         for b in range(NBLK):
-            matmul_dr(1, 1, b)
+            matmul_dr(1, 1, b, (1,))
+        weight_grad(2, 1)
         for j in range(2):
             dn_banks[1, j] = (bank(), bank())
         for b in range(NBLK):

import math
from contextlib import ExitStack

import concourse.mybir as mybir
from concourse.masks import make_identity

B, S, NS, DS, H = 8, 128, 2, 512, 1024
D = NS * DS
T = B * S
FLOPS = 2 * NS * T * DS * 2 * H + 2 * NS * T * DS * H
ROPE_BASE = 10000.0

F32 = mybir.dt.float32
BF16 = mybir.dt.bfloat16
I32 = mybir.dt.int32
U32 = mybir.dt.uint32
U8 = mybir.dt.uint8
E4 = mybir.dt.float8_e4m3fn_x4
E5 = mybir.dt.float8_e5m2_x4
ALU = mybir.AluOpType
ACT = mybir.ActivationFunctionType

P = 128
PACK = 4
KP = P * PACK
NBLK = DS // P
GROUPS = T // KP
CHUNKS = GROUPS * NS * (H // KP)
STEPS = 2 * CHUNKS
W_TILES = 2 * NS * (H // KP)
DG, DU = 0, 1

SLOTS = 5
DR_SLOT = (0, 2)
X_SLOT = (3, 1)


def tile_mopn_layer_pa_v_kernel(tc, x, norm_w, Wg, Wu, zg, zu, rstd, grad_out, out_0, out_1):
    nc = tc.nc
    by_token = "b s n h -> (b s) (n h)"
    tokens = "(g p j) w -> g p j w"
    zg_v = zg.rearrange(by_token).rearrange(tokens, p=P, j=PACK)
    zu_v = zu.rearrange(by_token).rearrange(tokens, p=P, j=PACK)
    go_v = grad_out.rearrange(by_token).rearrange(tokens, p=P, j=PACK)
    x_v = x.rearrange("b s d -> (b s) d").rearrange(tokens, p=P, j=PACK)
    dx_v = out_0.rearrange("b s d -> (b s) d").rearrange(tokens, p=P, j=PACK)
    weights = (Wg, Wu)

    with ExitStack() as ctx:
        keep = ctx.enter_context(tc.tile_pool(name="keep", bufs=1))
        flow = ctx.enter_context(tc.tile_pool(name="flow", bufs=2))
        psum = ctx.enter_context(tc.psum_pool(name="psum", bufs=8))
        ctx.enter_context(tc.manual_schedule())

        def bank():
            return psum.tile([P, KP], F32, name="bank", tag="bank")

        def work():
            return flow.tile([P, 2, KP], F32, name="work", tag="work", bufs=9)

        def grouped():
            return flow.tile([P, KP * PACK], BF16, name="grouped", tag="grouped", bufs=7, align_bytes=64)

        def quantize(src, fmt, tag, bufs):
            codes = flow.tile([P, KP], U32, name=tag, tag=tag, bufs=bufs, align_bytes=64)
            scales = flow.tile([P, KP], U8, name=tag + "_s", tag=tag + "_s", bufs=bufs, align_bytes=64)
            nc.vector.quantize_mx(out=codes[:].bitcast(fmt), scales=scales[:], in_=src[:])
            return codes, scales

        ident = keep.tile([P, P], F32, name="ident")
        ident16 = keep.tile([P, P], BF16, name="ident16")
        rs_half = keep.tile([P, GROUPS, PACK], F32, name="rs_half")
        rs = keep.tile([P, GROUPS, PACK], F32, name="rs")
        rs_sq = keep.tile([P, GROUPS, PACK], F32, name="rs_sq")
        tables = keep.tile([P, NBLK, SLOTS, P], F32, name="tables")
        sums = keep.tile([P, GROUPS * PACK, 8], F32, name="sums")

        xs, zgs, zus, gos, go_banks = {}, {}, {}, {}, {}
        common, slope, dgs, dus = {}, {}, {}, {}
        dz_grouped, dz_q, tok_grouped, tok_q = {}, {}, {}, {}
        raw_w, w_grouped, w_q = {}, {}, {}
        xhat, x_banks, r_terms, r_banks, r_grouped, r_q = {}, {}, {}, {}, {}, {}
        dr_banks, dn_terms, dn_banks, dx_rows = {}, {}, {}, {}

        def place(i):
            c, pair = divmod(i, 2)
            return c // 4, slice(2 * pair, 2 * pair + 2), slice(c % 4 * KP, (c % 4 + 1) * KP)

        def zg_tile():
            return flow.tile([P, 2, KP], F32, name="zg", tag="zg", bufs=3)

        def load_zg(i):
            g, js, cols = place(i)
            zgs[i] = zg_tile()
            nc.sync.dma_start(out=zgs[i][:], in_=zg_v[g, :, js, cols])

        def load_go(i):
            g, js, cols = place(i)
            gos[i] = flow.tile([P, 2, KP], BF16, name="go", tag="go")
            nc.sync.dma_start(out=gos[i][:], in_=go_v[g, :, js, cols])

        def load_zu(i):
            g, js, cols = place(i)
            zus[i] = flow.tile([P, 2, KP], F32, name="zu", tag="zu", bufs=3)
            nc.sync.dma_start(out=zus[i][:], in_=zu_v[g, :, js, cols])

        def load_x(g):
            xs[g] = keep.tile([P, PACK, D], BF16, name="x%d" % g)
            nc.sync.dma_start(out=xs[g][:], in_=x_v[g])

        def load_w(k):
            n, h, which = k // 4, k % 4 // 2, k % 2
            raw_w[k] = flow.tile([P, NBLK, KP], BF16, name="raw_w", tag="raw_w")
            w_by_block = weights[which][n].rearrange("(b p) f -> p b f", p=P)
            nc.sync.dma_start(out=raw_w[k][:], in_=w_by_block[:, :, h * KP : (h + 1) * KP])

        def turn_words(src, first):
            dst = bank()
            view = dst[:].rearrange("p (u r m) -> p u r m", u=2, r=2)
            words = src[:].bitcast(F32)
            for u in range(2):
                for r in range(2):
                    nc.tensor.transpose(view[:, u, r, :], words[:, first + r, u : 2 * P : 2], ident[:])
            return dst

        def empty_words(dst, half, src):
            out = dst[:].bitcast(F32).rearrange("p (h m u) -> p h m u", h=2, u=2)[:, half]
            nc.scalar.copy(out=out, in_=src[:].rearrange("p (u m) -> p m u", u=2))

        def turn_w(k):
            w_grouped[k] = grouped()
            for half in range(2):
                empty_words(w_grouped[k], half, turn_words(raw_w[k], 2 * half))

        def quantize_w(k):
            w_q[k] = quantize(w_grouped[k], E4, "w_q", W_TILES)

        def activations(i):
            common[i], slope[i] = work(), work()
            nc.scalar.activation(out=common[i][:], in_=zgs[i][:], func=ACT.Tanh, scale=-0.5)
            nc.scalar.activation(out=slope[i][:], in_=zgs[i][:], func=ACT.Silu, scale=-1.0)

        def move_go(i):
            go_banks[i] = psum.tile([P, 2, KP], BF16, name="bank", tag="bank")
            for r in range(2):
                nc.tensor.matmul(go_banks[i][:, r, :], lhsT=ident16[:], rhs=gos[i][:, r, :], start=True, stop=True)

        def gate_common(dst, go):
            nc.vector.scalar_tensor_tensor(out=dst, in0=dst, scalar=1.0, in1=go, op0=ALU.subtract, op1=ALU.mult)

        def gate_du(i):
            dus[i] = flow.tile([P, 2, KP], BF16, name="du", tag="du")
            nc.vector.scalar_tensor_tensor(out=dus[i][:], in0=common[i][:], scalar=-1.0, in1=zgs[i][:], op0=ALU.mult, op1=ALU.mult)

        def gate_slope(i):
            nc.vector.scalar_tensor_tensor(out=slope[i][:], in0=slope[i][:], scalar=1.0, in1=zus[i][:], op0=ALU.subtract, op1=ALU.mult)

        def gate_dg(i):
            c, pair = divmod(i, 2)
            if pair == 0:
                dgs[c] = flow.tile([P, PACK, KP], BF16, name="dg", tag="dg")
            nc.gpsimd.tensor_tensor(out=dgs[c][:, 2 * pair : 2 * pair + 2, :], in0=common[i][:], in1=slope[i][:], op=ALU.mult)

        def turn_dz(i, which):
            c, pair = divmod(i, 2)
            src = turn_words(dgs[c], 2 * pair) if which == DG else turn_words(dus[i], 0)
            if pair == 0:
                dz_grouped[c, which] = grouped()
            empty_words(dz_grouped[c, which], pair, src)

        def quantize_dz(c, which):
            dz_q[c, which] = quantize(dz_grouped[c, which], E5, "dz_q", 6)

        def interleave(c, half):
            if half == 0:
                tok_grouped[c] = grouped()
            quads = slice(half * KP // 8, (half + 1) * KP // 8)
            nc.scalar.copy(
                out=tok_grouped[c][:].rearrange("p (q f j) -> p q j f", f=4, j=PACK)[:, quads],
                in_=dgs[c][:].rearrange("p j (q f) -> p q j f", f=4)[:, quads],
            )

        def quantize_tok(c):
            tok_q[c] = quantize(tok_grouped[c], E5, "tok_q", 6)

        def rotate(out, src, b, slot):
            shape = [P, 2, PACK, 4, 32]
            nc.vector.tensor_tensor(
                out=out.rearrange("p s (j a q) -> p s j a q", j=PACK, a=4),
                in0=src[:].rearrange("p (s j a q) -> p s j a q", s=1, j=PACK, a=4).to_broadcast(shape),
                in1=tables[:, b, slot : slot + 2, :].rearrange("p s (j a q) -> p s j a q", j=PACK, a=1).to_broadcast(shape),
                op=ALU.mult,
            )

        def add_turned(dst, first, second):
            nc.tensor.matmul(dst, lhsT=first, rhs=ident[:], start=True, stop=False, is_transpose=True)
            nc.tensor.matmul(dst, lhsT=second, rhs=ident[:], start=False, stop=True, is_transpose=True)

        def scale_x(u):
            g, b = divmod(u, NBLK)
            xhat[u] = work()[:].rearrange("p s (a c) -> p (s a) c", c=2 * P)
            dst = xhat[u].rearrange("p j (h c) -> p j h c", h=2)
            src = xs[g][:].rearrange("p j (h b c) -> p j h b c", h=2, c=P)
            for j in range(PACK):
                nc.scalar.activation(out=dst[:, j], in_=src[:, j, :, b, :], func=ACT.Copy, scale=rs[:, g, j : j + 1])

        def turn_x(u):
            x_banks[u] = (bank(), bank())
            for half in range(2):
                for j in range(PACK):
                    nc.tensor.transpose(x_banks[u][half][:, j * P : (j + 1) * P], xhat[u][:, j, half * P : (half + 1) * P], ident[:])

        def rotate_x(u, half):
            r_terms[u, half] = work()
            rotate(r_terms[u, half][:], x_banks[u][half], u % NBLK, X_SLOT[half])

        def add_r(u):
            r_banks[u] = (bank(), bank())
            for half in range(2):
                for j in range(PACK):
                    cols = slice(j * P, (j + 1) * P)
                    add_turned(r_banks[u][half][:, cols], r_terms[u, 0][:, 1 - half, cols], r_terms[u, 1][:, half, cols])
            r_grouped[u] = flow.tile([P, 2, KP], BF16, name="r_grouped", tag="r_grouped", align_bytes=64)
            for half in range(2):
                nc.scalar.copy(
                    out=r_grouped[u][:, half, :].rearrange("p (c j) -> p c j", j=PACK),
                    in_=r_banks[u][half][:].rearrange("p (j c) -> p c j", j=PACK),
                )

        def quantize_r(u):
            g, b = divmod(u, NBLK)
            if b == 0:
                codes = keep.tile([P, D], U32, name="r_codes%d" % g, align_bytes=64)
                scales = keep.tile([P, D], U8, name="r_scales%d" % g, align_bytes=64)
                r_q[g] = (codes, scales)
            cols = slice(2 * b * P, 2 * (b + 1) * P)
            nc.vector.quantize_mx(
                out=r_q[g][0][:, cols].bitcast(E4), scales=r_q[g][1][:, cols], in_=r_grouped[u][:].rearrange("p s c -> p (s c)")
            )

        def mx(acc, lhs, cols, rhs, start, stop):
            nc.tensor.matmul_mx(
                out=acc[:], lhsT=lhs[0][:, cols].bitcast(E4), lhsT_scale=lhs[1][:, cols],
                rhs=rhs[0][:].bitcast(E5), rhs_scale=rhs[1][:], start=start, stop=stop,
            )

        def matmul_dr(g, n, b, halves=(0, 1)):
            if 0 in halves:
                dr_banks[g, n, b] = bank()
            for h in halves:
                for which in (DU, DG):
                    mx(
                        dr_banks[g, n, b], w_q[4 * n + 2 * h + which], slice(b * P, (b + 1) * P), dz_q[4 * g + 2 * n + h, which],
                        (h, which) == (0, DU), (h, which) == (1, DG),
                    )

        def weight_grad(c, pair):
            n, h = divmod(c, 2)
            stage = work()
            for s in range(2):
                b = 2 * pair + s
                acc = bank()
                for g in range(GROUPS):
                    mx(acc, r_q[g], slice((2 * b + n) * P, (2 * b + n + 1) * P), tok_q[4 * g + c], g == 0, g == GROUPS - 1)
                nc.scalar.activation(out=stage[:, s, :], in_=acc[:], func=ACT.Copy, scale=0.5)
            dw_by_block = out_1[n].rearrange("(b p) f -> p b f", p=P)
            nc.sync.dma_start(out=dw_by_block[:, 2 * pair : 2 * pair + 2, h * KP : (h + 1) * KP], in_=stage[:])

        def rotate_dr(g, n, b):
            if b == 0:
                dn_terms[g, n] = flow.tile([P, NBLK, 2, KP], F32, name="dn_terms", tag="dn_terms")
            rotate(dn_terms[g, n][:, b], dr_banks[g, n, b], b, DR_SLOT[n])

        def add_dn_block(g, j, b):
            cols = slice(j * P, (j + 1) * P)
            for half in range(2):
                dst = dn_banks[g, j][half][:, b * P : (b + 1) * P]
                add_turned(dst, dn_terms[g, 0][:, b, half, cols], dn_terms[g, 1][:, b, 1 - half, cols])

        def add_dn(g, j):
            dn_banks[g, j] = (bank(), bank())
            for b in range(NBLK):
                add_dn_block(g, j, b)

        def total(g, j):
            return sums[:, PACK * g + j, 2:3]

        def row_sums(g, j):
            dx_rows[g, j] = work()
            for half in range(2):
                nc.vector.scalar_tensor_tensor(
                    out=dx_rows[g, j][:, half, :], in0=dn_banks[g, j][half][:], scalar=rs_sq[:, g, j : j + 1],
                    in1=xs[g][:, j, half * DS : (half + 1) * DS], op0=ALU.mult, op1=ALU.mult,
                    accum_out=sums[:, PACK * g + j, half : half + 1],
                )

        def join_sums(g, j):
            halves = sums[:, PACK * g + j, :]
            nc.vector.tensor_scalar(out=total(g, j), in0=halves[:, 0:1], scalar1=halves[:, 1:2], scalar2=None, op0=ALU.add)

        def finish_row(g, j):
            for half in range(2):
                nc.vector.scalar_tensor_tensor(
                    out=dx_rows[g, j][:, half, :], in0=xs[g][:, j, half * DS : (half + 1) * DS], scalar=total(g, j),
                    in1=dn_banks[g, j][half][:], op0=ALU.mult, op1=ALU.add,
                )

        def store_row(g, j):
            row = dx_rows[g, j][:].rearrange("p s c -> p (s c)")
            nc.scalar.activation(out=row, in_=row, func=ACT.Copy, scale=rs_half[:, g, j : j + 1])
            nc.sync.dma_start(out=dx_v[g, :, j, :], in_=row)

        def scale_row(g, j):
            dx_rows[g, j] = work()
            for half in range(2):
                nc.scalar.activation(
                    out=dx_rows[g, j][:, half, :], in_=dn_banks[g, j][half][:], func=ACT.Copy, scale=rs_half[:, g, j : j + 1]
                )

        def scaled_row_sum(g, j):
            products = work()
            nc.vector.scalar_tensor_tensor(
                out=products[:].rearrange("p s c -> p (s c)"), in0=dx_rows[g, j][:].rearrange("p s c -> p (s c)"),
                scalar=rs_sq[:, g, j : j + 1], in1=xs[g][:, j, :], op0=ALU.mult, op1=ALU.mult, accum_out=total(g, j),
            )

        def finish_scaled_row(g, j, pieces):
            row = dx_rows[g, j][:].rearrange("p s c -> p (s c)")
            for k in range(pieces):
                cols = slice(k * D // pieces, (k + 1) * D // pieces)
                nc.vector.scalar_tensor_tensor(
                    out=row[:, cols], in0=xs[g][:, j, cols], scalar=total(g, j), in1=row[:, cols], op0=ALU.mult, op1=ALU.add
                )
                nc.sync.dma_start(out=dx_v[g, :, j, cols], in_=row[:, cols])

        w_rows = keep.tile([P, P], BF16, name="w_rows")
        small = work()
        freq_row, w_rows32, pos = small[:, 0, 0:P], small[:, 0, P : 2 * P], small[:, 0, 2 * P : 3 * P]
        freq_col = keep.tile([P, 1], F32, name="freq_col")
        nc.vector.memset(w_rows[:], 0.0)
        nc.vector.memset(freq_row[:, 0:1], 1.0)
        zgs[0] = zg_tile()
        nc.sync.dma_start(out=zgs[0][:, 0, :], in_=zg_v[0, :, 0, 0:KP])
        load_go(0)
        nc.sync.dma_start(out=zgs[0][:, 1, :], in_=zg_v[0, :, 1, 0:KP])
        nc.sync.dma_start(out=w_rows[0 : D // P, :], in_=norm_w.rearrange("(c p) -> c p", p=P))
        load_zu(0)
        nc.sync.dma_start(out=rs[:], in_=rstd.rearrange("b s -> (b s)").rearrange("(g p j) -> p g j", p=P, j=PACK))
        load_zg(1)
        load_go(1)
        load_x(0)
        load_zu(1)
        nc.gpsimd.iota(pos, pattern=[[1, PACK], [PACK, 32]], base=0, channel_multiplier=0, allow_small_or_imprecise_dtypes=True)
        make_identity(nc, ident[:])
        nc.gpsimd.tensor_copy(out=ident16[:], in_=ident[:])
        decay = math.log(ROPE_BASE) / DS
        for k in range(7):
            filled = 2**k
            nc.vector.tensor_scalar(
                out=freq_row[:, filled : 2 * filled], in0=freq_row[:, 0:filled], scalar1=math.exp(-decay * filled), scalar2=None, op0=ALU.mult
            )
        freq_bank, w_bank = bank(), bank()
        nc.tensor.transpose(freq_bank[:, 0:P], freq_row, ident[:])
        nc.vector.tensor_copy(out=freq_col[:], in_=freq_bank[:, 0:1])
        common[0], slope[0] = work(), work()
        for func, scale, dst, r in (
            (ACT.Silu, -1.0, slope[0], 0), (ACT.Tanh, -0.5, common[0], 0), (ACT.Tanh, -0.5, common[0], 1), (ACT.Silu, -1.0, slope[0], 1)
        ):
            nc.scalar.activation(out=dst[:, r, :], in_=zgs[0][:, r, :], func=func, scale=scale)
        trig = work()
        turns, whole = trig[:, 0, :], trig[:, 1, :].bitcast(I32)
        for b in range(NBLK):
            nc.vector.tensor_scalar(
                out=turns[:, b * P : (b + 1) * P], in0=pos, scalar1=freq_col[:],
                scalar2=math.exp(-decay * P * b) / (2 * math.pi), op0=ALU.mult, op1=ALU.mult,
            )
        nc.vector.tensor_copy(out=whole, in_=turns)
        gate_common(common[0][:, 0:1], gos[0][:, 0:1])
        nc.vector.tensor_tensor(out=turns, in0=turns, in1=whole, op=ALU.subtract)
        gate_common(common[0][:, 1:2], gos[0][:, 1:2])
        nc.vector.tensor_copy(out=w_rows32, in_=w_rows[:])
        nc.tensor.transpose(w_bank[:, 0:P], w_rows32, ident[:])
        sin, cos = small[:, 1, :], trig[:, 1, :]
        nc.scalar.activation(out=cos, in_=turns, func=ACT.Abs)
        nc.scalar.activation(out=sin, in_=turns, func=ACT.Sin, scale=2 * math.pi)
        nc.scalar.activation(out=cos, in_=cos, func=ACT.Sin, scale=-2 * math.pi, bias=math.pi / 2)

        def fill_tables():
            for slot, wave, sign, half in ((1, sin, -1.0, 1), (3, sin, 1.0, 0), (0, cos, 1.0, 0), (2, cos, 1.0, 1), (4, cos, 1.0, 0)):
                gain = w_bank[:, NBLK * half : NBLK * (half + 1)].rearrange("p (b a) -> p b a", a=1).to_broadcast([P, NBLK, P])
                nc.vector.scalar_tensor_tensor(
                    out=tables[:, :, slot, :], in0=wave.rearrange("p (b c) -> p b c", c=P), scalar=sign, in1=gain, op0=ALU.mult, op1=ALU.mult
                )

        dr_at = {6: [(0, 0, 0), (0, 0, 1)], 7: [(0, 0, 2), (0, 0, 3)], 10: [(0, 1, b) for b in range(NBLK)], 15: [(1, 0, 0), (1, 0, 1)]}
        row_at = {11 + j: j for j in range(PACK)}
        r_at = {i: u for u, i in enumerate([i for i in range(1, STEPS) if i not in dr_at][: GROUPS * NBLK])}
        grad_at = {13: 0, 14: 1}

        def feed(i):
            if i in r_at:
                turn_x(r_at[i])
            for key in dr_at.get(i, []):
                matmul_dr(*key)
            if i in row_at:
                add_dn(0, row_at[i])

        for i in range(STEPS):
            last = i == STEPS - 1
            c, pair = divmod(i, 2)
            if i + 2 < STEPS:
                load_zg(i + 2)
            if i < W_TILES:
                load_w(i)
            if i == 2:
                load_x(1)
            if not last:
                activations(i + 1)
            if i == 0:
                scale_x(0)
            if not last:
                move_go(i + 1)
            if i + 2 < STEPS:
                load_go(i + 2)
                load_zu(i + 2)
            if i - 1 in row_at:
                store_row(0, row_at[i - 1])
            if i - 1 in r_at:
                add_r(r_at[i - 1])
            if i >= 1:
                turn_dz(i - 1, DG)
            if last:
                for b in range(2, NBLK):
                    matmul_dr(1, 0, b)
            if 1 <= i <= W_TILES:
                turn_w(i - 1)
            gate_du(i)
            turn_dz(i, DU)
            if c >= 1:
                interleave(c - 1, pair)
            if i + 2 in r_at:
                scale_x(r_at[i + 2])
            if i - 2 in r_at:
                quantize_r(r_at[i - 2])
            if c >= 1 and pair == 1:
                quantize_dz(c - 1, DG)
            if 2 <= i < W_TILES + 2:
                quantize_w(i - 2)
            if c >= 1 and pair == 0:
                quantize_dz(c - 1, DU)
            if c >= 2 and pair == 0:
                quantize_tok(c - 2)
            if i == 0:
                nc.vector.tensor_scalar(out=rs_half[:], in0=rs[:], scalar1=0.5, scalar2=None, op0=ALU.mult)
                nc.vector.scalar_tensor_tensor(out=rs_sq[:], in0=rs[:], scalar=-1.0 / D, in1=rs[:], op0=ALU.mult, op1=ALU.mult)
            if i in grad_at:
                for block_pair in range(2):
                    weight_grad(grad_at[i], block_pair)
            gate_slope(i)
            gate_dg(i)
            if i == 0:
                fill_tables()
            rotations = [(rotate_x, (r_at[i], half)) for half in range(2)] if i in r_at else []
            rotations = rotations + [(rotate_dr, key) for key in dr_at.get(i, [])]
            if i in row_at:
                row_sums(0, row_at[i])
            for func, key in rotations[:-1]:
                func(*key)
            if i in row_at:
                gate_common(common[i + 1][:, 0:1], go_banks[i + 1][:, 0:1])
                join_sums(0, row_at[i])
                gate_common(common[i + 1][:, 1:2], go_banks[i + 1][:, 1:2])
            elif not last:
                gate_common(common[i + 1][:], go_banks[i + 1][:])
            for func, key in rotations[-1:]:
                func(*key)
            if i in row_at:
                finish_row(0, row_at[i])
            feed(i + 1)

        for b in range(NBLK):
            matmul_dr(1, 1, b, (0,))
        turn_dz(STEPS - 1, DG)
        for half in range(2):
            interleave(CHUNKS - 1, half)
        rotate_dr(1, 0, 2)
        quantize_tok(CHUNKS - 2)
        quantize_dz(CHUNKS - 1, DU)
        quantize_dz(CHUNKS - 1, DG)
        rotate_dr(1, 0, 3)
        weight_grad(2, 0)
        for b in range(NBLK):
            matmul_dr(1, 1, b, (1,))
        weight_grad(2, 1)
        for j in range(2):
            dn_banks[1, j] = (bank(), bank())
        for b in range(NBLK):
            rotate_dr(1, 1, b)
            if b == 0:
                quantize_tok(CHUNKS - 1)
            for j in range(2):
                add_dn_block(1, j, b)
        scale_row(1, 1)
        weight_grad(3, 0)
        add_dn(1, 2)
        add_dn(1, 3)
        row_sums(1, 0)
        join_sums(1, 0)
        scaled_row_sum(1, 1)
        finish_row(1, 0)
        scale_row(1, 2)
        store_row(1, 0)
        scale_row(1, 3)
        finish_scaled_row(1, 1, 1)
        weight_grad(3, 1)
        scaled_row_sum(1, 2)
        scaled_row_sum(1, 3)
        finish_scaled_row(1, 2, 1)
        finish_scaled_row(1, 3, 2)
